import numpy as np
import ml_dtypes


def mxq(x, axis, fmt="e4m3"):
    dtype, down = {"e4m3": (ml_dtypes.float8_e4m3fn, 7), "e5m2": (ml_dtypes.float8_e5m2, 14)}[fmt]
    v = np.moveaxis(np.asarray(x, np.float32).astype(ml_dtypes.bfloat16).astype(np.float64), axis, -1)
    blocks = v.reshape(v.shape[:-1] + (-1, 32))
    amax = np.abs(blocks).max(-1, keepdims=True)
    byte = np.maximum(np.where(amax > 0, np.frexp(amax)[1] - 1 + 127, 0) - down, 1)
    scale = np.exp2(byte - 127.0)
    codes = (blocks / scale).astype(np.float32).astype(dtype).astype(np.float64)
    return np.moveaxis((codes * scale).reshape(v.shape), -1, axis)


WIDE = False


def mx_kscale(k):
    if not WIDE:
        return np.ones(k)
    levels = np.array([10, -10, 5, -5, 0])
    a = np.random.permutation(np.resize(levels, k // 512 * 4)).reshape(k // 512, 4)
    idx = np.arange(k)
    return np.exp2(a[idx // 512, idx % 128 // 32])


BF16 = ml_dtypes.bfloat16


def bf(x):
    return np.asarray(x, np.float32).astype(BF16)


def f64(x):
    return np.asarray(x).astype(np.float64)


B, C, HID, H, W = 2, 1024, 64, 32, 32
N_P, N_H, N_F, N_U, N_L = 7, 3, 2, 4, 2
EPS = 1e-5


def setup_inputs():
    s = mx_kscale(C)
    off = 0.5 * np.random.standard_normal((1, C, 1, 1))
    return {
        "p_nodes": bf(np.random.standard_normal((N_P, B, HID, H, W))),
        "h_nodes": bf(np.random.standard_normal((N_H, B, HID, H, W))),
        "f_nodes": bf(np.random.standard_normal((N_F, B, HID, H, W))),
        "xp": bf((np.random.standard_normal((B, C, H, W)) + off) * s[None, :, None, None]),
        "h_att": bf(np.random.uniform(0.0, 1.0, (N_H, B, 1, H, W))),
        "Wu": bf(np.random.standard_normal((N_U * HID, C)) / np.sqrt(C) / s[None, :]),
        "Wl": bf(np.random.standard_normal((N_L * HID, C)) / np.sqrt(C) / s[None, :]),
        "gamma_u": bf(1.0 + 0.1 * np.random.standard_normal(N_U * HID)),
        "beta_u": bf(0.1 * np.random.standard_normal(N_U * HID)),
        "gamma_l": bf(1.0 + 0.1 * np.random.standard_normal(N_L * HID)),
        "beta_l": bf(0.1 * np.random.standard_normal(N_L * HID)),
    }


def conv_bn_relu(x, Wc, gamma, beta):
    y = (mxq(Wc, 1, "e4m3") @ mxq(x, 1, "e4m3").reshape(B, C, H * W)).reshape(B, -1, H, W)
    m = y.mean(axis=(0, 2, 3), keepdims=True)
    v = y.var(axis=(0, 2, 3), keepdims=True)
    y = (y - m) / np.sqrt(v + EPS)
    y = y * gamma[None, :, None, None] + beta[None, :, None, None]
    return np.maximum(y, 0.0)


def reference(p_nodes, h_nodes, f_nodes, xp, h_att, Wu, Wl, gamma_u, beta_u, gamma_l, beta_l):
    p_nodes, h_nodes, xp, h_att = f64(p_nodes), f64(h_nodes), f64(xp), f64(h_att)
    du = conv_bn_relu(h_att[1] * xp, f64(Wu), f64(gamma_u), f64(beta_u))
    dl = conv_bn_relu(h_att[2] * xp, f64(Wl), f64(gamma_l), f64(beta_l))
    du4 = du.reshape(B, N_U, HID, H, W).transpose(1, 0, 2, 3, 4)
    dl2 = dl.reshape(B, N_L, HID, H, W).transpose(1, 0, 2, 3, 4)
    p0 = 0.5 * (h_nodes[0] + p_nodes[0])
    p_up = 0.5 * (p_nodes[1:1 + N_U] + du4)
    p_low = 0.5 * (p_nodes[1 + N_U:N_P] + dl2)
    return np.concatenate([p0[None], p_up, p_low], axis=0)

@@ -1,0 +1,315 @@
+from contextlib import ExitStack
+
+import concourse.mybir as mybir
+from concourse.masks import make_identity
+
+FLOPS = 2 * 384 * 1024 * 2048
+BYTES = 10757632
+
+BF16 = mybir.dt.bfloat16
+F32 = mybir.dt.float32
+U32 = mybir.dt.uint32
+U8 = mybir.dt.uint8
+FP8X4 = mybir.dt.float8_e4m3fn_x4
+ACT = mybir.ActivationFunctionType
+ALU = mybir.AluOpType
+
+P = 128
+EPS = 1e-5
+NPIX = 2048
+V_UNITS = (0, 1, 4, 8, 11, 14)
+LOOKAHEAD = 2
+
+
+def tile_gnn_kernel(tc, p_nodes, h_nodes, f_nodes, xp, h_att, Wu, Wl, gamma_u, beta_u, gamma_l, beta_l, out):
+    nc = tc.nc
+    with ExitStack() as ctx:
+        keep = ctx.enter_context(tc.tile_pool(name="keep", bufs=1))
+        prods = ctx.enter_context(tc.tile_pool(name="prods", bufs=3))
+        ps_att = ctx.enter_context(tc.psum_pool(name="ps_att", bufs=4))
+        ps_y = ctx.enter_context(tc.psum_pool(name="ps_y", bufs=4))
+        ctx.enter_context(tc.manual_schedule())
+
+        xr = [keep.tile([P, 4, 512], BF16, name="xr%d" % i) for i in range(8)]
+        xg = [keep.tile([P, 512, 4], BF16, name="xg%d" % i) for i in range(8)]
+        xc = [keep.tile([P, 512], U32, name="xc%d" % k, align_bytes=64) for k in range(16)]
+        xs = [keep.tile([P, 512], U8, name="xs%d" % k, align_bytes=64) for k in range(16)]
+        w_sb = [keep.tile([P, 1024], BF16, name="w_sb%d" % t) for t in range(3)]
+        wg = [keep.tile([P, 1024], BF16, name="wg%d" % t, align_bytes=64) for t in range(3)]
+        wc = [keep.tile([P, 256], U32, name="wc%d" % t, align_bytes=64) for t in range(3)]
+        ws = [keep.tile([P, 256], U8, name="ws%d" % t, align_bytes=64) for t in range(3)]
+        y_sb = [keep.tile([P, NPIX], F32, name="y_sb%d" % t) for t in range(3)]
+        o_sb = [keep.tile([P, NPIX], F32, name="o_sb%d" % t) for t in range(3)]
+        pn = [keep.tile([P, 2, 1024], BF16, name="pn%d" % t) for t in range(3)]
+        sums = [keep.tile([P, 4], F32, name="sums%d" % t) for t in range(3)]
+        junk4 = [keep.tile([P, 4], F32, name="junk4_%d" % t) for t in range(3)]
+        negmean = [keep.tile([P, 1], F32, name="negmean%d" % t) for t in range(3)]
+        m2 = [keep.tile([P, 1], F32, name="m2_%d" % t) for t in range(3)]
+        rstd = [keep.tile([P, 1], F32, name="rstd%d" % t) for t in range(3)]
+        scl = [keep.tile([P, 1], F32, name="scl%d" % t) for t in range(3)]
+        bia = [keep.tile([P, 1], F32, name="bia%d" % t) for t in range(3)]
+        h0 = keep.tile([P, 1024], BF16, name="h0")
+        p0 = keep.tile([P, 1024], BF16, name="p0")
+        o0 = keep.tile([P, 1024], F32, name="o0")
+        ident_f = keep.tile([P, P], F32, name="ident_f")
+        ident_b = keep.tile([P, P], BF16, name="ident_b")
+        half_i = keep.tile([P, P], BF16, name="half_i")
+        a0 = keep.tile([P, 32], BF16, name="a0")
+        a1 = keep.tile([P, 32, 4], BF16, name="a1")
+        att_p = keep.tile([P, P], BF16, name="att_p")
+        g0 = keep.tile([P, P], BF16, name="g0")
+        g1 = keep.tile([P, P], BF16, name="g1")
+        gb = keep.tile([P, 6], F32, name="gb")
+        eps_t = keep.tile([P, 1], F32, name="eps_t")
+        warm = keep.tile([P, 1], F32, name="warm")
+
+        nc.vector.memset(eps_t[:], EPS)
+        nc.scalar.activation(out=warm[:], in_=eps_t[:], func=ACT.Abs_reciprocal_sqrt)
+        nc.vector.memset(g0[:], 0.0)
+        nc.scalar.dma_start(out=a0[:], in_=h_att[1:3].rearrange("a b o h w -> (a b o h) w"))
+        nc.scalar.dma_start(out=g0[0:2, :], in_=gamma_u.rearrange("(r c) -> r c", c=P))
+        nc.scalar.dma_start(out=g0[2:3, :], in_=gamma_l.rearrange("(r c) -> r c", c=P))
+        nc.scalar.dma_start(out=g0[3:5, :], in_=beta_u.rearrange("(r c) -> r c", c=P))
+        nc.scalar.dma_start(out=g0[5:6, :], in_=beta_l.rearrange("(r c) -> r c", c=P))
+
+        def load_x(i):
+            s, g = divmod(i, 2)
+            b, h = divmod(s, 2)
+            rows = xp[b, 512 * g : 512 * g + 512].rearrange("(p j) h w -> p j (h w)", j=4)
+            nc.sync.dma_start(out=xr[i][:], in_=rows[:, :, 512 * h : 512 * h + 512])
+
+        def load_w(t):
+            for jj in range(2):
+                rows = Wu[P * t + 64 * jj : P * t + 64 * jj + 64, :] if t < 2 else Wl[64 * jj : 64 * jj + 64, :]
+                nc.sync.dma_start(out=w_sb[t][jj:P:2, :], in_=rows)
+
+        def load_p(t):
+            for jj in range(2):
+                nc.sync.dma_start(out=pn[t][jj:P:2, :, :], in_=p_nodes[1 + 2 * t + jj].rearrange("b c h w -> c b (h w)"))
+
+        for i in range(3):
+            load_x(i)
+        for t in range(3):
+            load_w(t)
+        for i in range(3, 8):
+            load_x(i)
+        load_p(0)
+        load_p(1)
+        nc.sync.dma_start(out=h0[:], in_=h_nodes[0].rearrange("b c h w -> (b c) (h w)"))
+        nc.sync.dma_start(out=p0[:], in_=p_nodes[0].rearrange("b c h w -> (b c) (h w)"))
+        load_p(2)
+
+        make_identity(nc, ident_b[:])
+        make_identity(nc, ident_f[:])
+        nc.vector.tensor_copy(out=a1[:], in_=a0[:].unsqueeze(2).to_broadcast([P, 32, 4]))
+        att_t = ps_att.tile([P, 1024], BF16, name="att_t", tag="att")
+        nc.tensor.transpose(att_t[:, 0:P], a1[:].rearrange("p w j -> p (w j)"), ident_b[:])
+        nc.vector.tensor_copy(out=att_p[:], in_=att_t[:, 0:P])
+        nc.vector.tensor_copy(
+            out=g1[:].rearrange("r (c jj) -> r c jj", jj=2), in_=g0[:].rearrange("r (jj c) -> r c jj", jj=2)
+        )
+        g_t = ps_att.tile([P, 1024], BF16, name="g_t", tag="att")
+        nc.tensor.transpose(g_t[:, 0:P], g1[:], ident_b[:])
+        nc.vector.tensor_scalar(out=gb[:], in0=g_t[:, 0:6], scalar1=0.5, scalar2=None, op0=ALU.mult)
+        nc.vector.tensor_scalar(out=half_i[:], in0=ident_f[:], scalar1=0.5, scalar2=None, op0=ALU.mult)
+
+        halves = [(a, s, g) for a in range(2) for s in range(4) for g in range(2)]
+        att_bank = {}
+        prod = {}
+        y_bank = {}
+
+        def o_tiles(a):
+            return (0, 1) if a == 0 else (2,)
+
+        def regroup(engine_copy, u):
+            i, q = divmod(u, 2)
+            dst = xg[i][:, 256 * q : 256 * q + 256, :].rearrange("p (c i) t -> p c t i", i=4)
+            src = xr[i][:, :, 256 * q : 256 * q + 256].rearrange("p t (c i) -> p c t i", i=4)
+            engine_copy(out=dst, in_=src)
+
+        def scalar_units(i):
+            if i < 8:
+                for q in range(2):
+                    if 2 * i + q not in V_UNITS:
+                        regroup(nc.scalar.copy, 2 * i + q)
+
+        def spread_att(a, s):
+            for q in range(2):
+                bank = ps_att.tile([P, 1024], BF16, name="att_bank", tag="att")
+                for r in range(8):
+                    row = 64 * a + 16 * s + 8 * q + r
+                    nc.tensor.transpose(
+                        bank[:, P * r : P * r + P], att_p[:, row : row + 1].to_broadcast([P, P]), ident_b[:]
+                    )
+                att_bank[(a, s, q)] = bank
+
+        def multiply(k, q):
+            a, s, g = halves[k]
+            if q == 0:
+                prod[k] = prods.tile([P, 2048], BF16, name="prod", tag="prod", align_bytes=64)
+            nc.vector.tensor_tensor(
+                out=prod[k][:, 1024 * q : 1024 * q + 1024],
+                in0=xg[2 * s + g][:, 256 * q : 256 * q + 256, :].rearrange("p w j -> p (w j)"),
+                in1=att_bank[(a, s, q)][:],
+                op=ALU.mult,
+            )
+
+        def quantise(k):
+            nc.vector.quantize_mx(out=xc[k][:].bitcast(FP8X4), scales=xs[k][:], in_=prod[k][:])
+
+        def w_transpose(t):
+            bank = ps_y.tile([P, 512], F32, name="w_bank", tag="y")
+            words = w_sb[t][:].bitcast(F32)
+            for g in range(2):
+                for u in range(2):
+                    nc.tensor.transpose(
+                        bank[:, P * (2 * g + u) : P * (2 * g + u) + P],
+                        words[:, 256 * g + u : 256 * g + 256 : 2],
+                        ident_f[:],
+                    )
+            y_bank[("w", t)] = bank
+
+        def w_copy(t):
+            nc.scalar.copy(
+                out=wg[t][:].bitcast(F32).rearrange("p (g o u) -> p g o u", g=2, u=2),
+                in_=y_bank[("w", t)][:].rearrange("p (g u o) -> p g o u", g=2, u=2),
+            )
+
+        def w_quantise(t):
+            nc.vector.quantize_mx(out=wc[t][:].bitcast(FP8X4), scales=ws[t][:], in_=wg[t][:])
+
+        def convolve(a, s):
+            for t in o_tiles(a):
+                bank = ps_y.tile([P, 512], F32, name="y_bank", tag="y")
+                for g in range(2):
+                    k = 8 * a + 2 * s + g
+                    nc.tensor.matmul_mx(
+                        out=bank[:],
+                        lhsT=wc[t][:, P * g : P * g + P].bitcast(FP8X4),
+                        lhsT_scale=ws[t][:, P * g : P * g + P],
+                        rhs=xc[k][:].bitcast(FP8X4),
+                        rhs_scale=xs[k][:],
+                        start=(g == 0),
+                        stop=(g == 1),
+                    )
+                y_bank[(t, s)] = bank
+
+        def take_out(a, s):
+            for t in o_tiles(a):
+                nc.scalar.activation(
+                    out=y_sb[t][:, 512 * s : 512 * s + 512],
+                    in_=y_bank[(t, s)][:],
+                    func=ACT.Identity,
+                    accum_out=sums[t][:, s : s + 1],
+                )
+
+        def statistics(t):
+            nc.scalar.activation(
+                out=junk4[t][:], in_=sums[t][:], func=ACT.Identity, scale=-1.0 / NPIX, accum_out=negmean[t][:]
+            )
+            nc.scalar.activation(
+                out=o_sb[t][:], in_=y_sb[t][:], func=ACT.Square, bias=negmean[t][:], accum_out=m2[t][:]
+            )
+            nc.scalar.activation(
+                out=rstd[t][:], in_=m2[t][:], func=ACT.Abs_reciprocal_sqrt, scale=1.0 / NPIX, bias=eps_t[:]
+            )
+            nc.scalar.activation(out=scl[t][:], in_=gb[:, t : t + 1], func=ACT.Identity, scale=rstd[t][:])
+            nc.scalar.activation(
+                out=bia[t][:], in_=negmean[t][:], func=ACT.Identity, scale=scl[t][:], bias=gb[:, 3 + t : 4 + t]
+            )
+
+        def relu(t, lo, n):
+            nc.scalar.activation(
+                out=y_sb[t][:, lo : lo + n], in_=y_sb[t][:, lo : lo + n], func=ACT.Relu, scale=scl[t][:], bias=bia[t][:]
+            )
+
+        def average(t, lo, n):
+            b, w0 = divmod(lo, 1024)
+            nc.vector.scalar_tensor_tensor(
+                out=o_sb[t][:, lo : lo + n],
+                in0=pn[t][:, b, w0 : w0 + n],
+                scalar=0.5,
+                in1=y_sb[t][:, lo : lo + n],
+                op0=ALU.mult,
+                op1=ALU.add,
+            )
+            for jj in range(2):
+                nc.sync.dma_start(
+                    out=out[1 + 2 * t + jj, b].rearrange("c h w -> c (h w)")[:, w0 : w0 + n],
+                    in_=o_sb[t][jj:P:2, lo : lo + n],
+                )
+
+        def node0_sum(h):
+            bank = ps_y.tile([P, 512], F32, name="o0_bank", tag="y")
+            nc.tensor.matmul(out=bank[:], lhsT=half_i[:], rhs=h0[:, 512 * h : 512 * h + 512], start=True, stop=False)
+            nc.tensor.matmul(out=bank[:], lhsT=half_i[:], rhs=p0[:, 512 * h : 512 * h + 512], start=False, stop=True)
+            y_bank[("o0", h)] = bank
+
+        def node0_out(h):
+            nc.scalar.copy(out=o0[:, 512 * h : 512 * h + 512], in_=y_bank[("o0", h)][:])
+
+        def fill(k):
+            if k == 1:
+                for t in range(3):
+                    w_transpose(t)
+                for t in range(3):
+                    w_copy(t)
+            if k == 3:
+                for t in range(3):
+                    w_quantise(t)
+            if k == 5:
+                take_out(0, 0)
+            if k == 7:
+                take_out(0, 1)
+            if k == 9:
+                take_out(0, 2)
+            if k == 10:
+                take_out(0, 3)
+                statistics(0)
+            if k == 11:
+                statistics(1)
+            if k == 12:
+                node0_sum(0)
+                node0_sum(1)
+                take_out(1, 0)
+                relu(0, 0, 1024)
+                relu(0, 1024, 1024)
+            if k == 13:
+                node0_out(0)
+                node0_out(1)
+                nc.sync.dma_start(out=out[0].rearrange("b c h w -> (b c) (h w)"), in_=o0[:])
+                relu(1, 0, 1024)
+            if k == 14:
+                take_out(1, 1)
+                relu(1, 1024, 1024)
+
+        spread_att(0, 0)
+        for i in range(LOOKAHEAD):
+            scalar_units(i)
+        for k in range(16):
+            a, s, g = halves[k]
+            scalar_units(k + LOOKAHEAD)
+            if g == 0 and k + 2 < 16:
+                spread_att(halves[k + 2][0], halves[k + 2][1])
+            for q in range(2):
+                if a == 0 and 2 * k + q in V_UNITS:
+                    regroup(nc.vector.tensor_copy, 2 * k + q)
+                if q == 1 and k > 0:
+                    quantise(k - 1)
+                multiply(k, q)
+            if k == 4:
+                convolve(0, 0)
+            if g == 0 and k >= 4:
+                convolve(halves[k - 2][0], halves[k - 2][1])
+            fill(k)
+        quantise(15)
+        convolve(1, 3)
+        take_out(1, 2)
+        take_out(1, 3)
+        statistics(2)
+        for t in range(2):
+            for b in range(2):
+                average(t, 1024 * b, 1024)
+        for c in range(4):
+            relu(2, 512 * c, 512)
+            average(2, 512 * c, 512)

@@ -18,6 +18,7 @@ P = 128
 EPS = 1e-5
 NPIX = 2048
 V_UNITS = (0, 1, 4, 8, 11, 14)
+G_PIX = 0
 LOOKAHEAD = 2
 
 
@@ -42,9 +43,13 @@ def tile_gnn_kernel(tc, p_nodes, h_nodes, f_nodes, xp, h_att, Wu, Wl, gamma_u, b
         o_sb = [keep.tile([P, NPIX], F32, name="o_sb%d" % t) for t in range(3)]
         pn = [keep.tile([P, 2, 1024], BF16, name="pn%d" % t) for t in range(3)]
         sums = [keep.tile([P, 4], F32, name="sums%d" % t) for t in range(3)]
-        junk4 = [keep.tile([P, 4], F32, name="junk4_%d" % t) for t in range(3)]
+        sqs = [keep.tile([P, 4], F32, name="sqs%d" % t) for t in range(3)]
+        junk_a = [keep.tile([P, 4], F32, name="junk_a%d" % t) for t in range(3)]
+        junk_b = [keep.tile([P, 4], F32, name="junk_b%d" % t) for t in range(3)]
+        negc = [keep.tile([P, 1], F32, name="negc%d" % t) for t in range(3)]
         negmean = [keep.tile([P, 1], F32, name="negmean%d" % t) for t in range(3)]
-        m2 = [keep.tile([P, 1], F32, name="m2_%d" % t) for t in range(3)]
+        msq = [keep.tile([P, 1], F32, name="msq%d" % t) for t in range(3)]
+        dsq = [keep.tile([P, 1], F32, name="dsq%d" % t) for t in range(3)]
         rstd = [keep.tile([P, 1], F32, name="rstd%d" % t) for t in range(3)]
         scl = [keep.tile([P, 1], F32, name="scl%d" % t) for t in range(3)]
         bia = [keep.tile([P, 1], F32, name="bia%d" % t) for t in range(3)]
@@ -54,29 +59,34 @@ def tile_gnn_kernel(tc, p_nodes, h_nodes, f_nodes, xp, h_att, Wu, Wl, gamma_u, b
         ident_f = keep.tile([P, P], F32, name="ident_f")
         ident_b = keep.tile([P, P], BF16, name="ident_b")
         half_i = keep.tile([P, P], BF16, name="half_i")
-        a0 = keep.tile([P, 32], BF16, name="a0")
-        a1 = keep.tile([P, 32, 4], BF16, name="a1")
-        att_p = keep.tile([P, P], BF16, name="att_p")
+        a0 = keep.tile([P, 64], BF16, name="a0")
+        a1 = keep.tile([P, 64, 4], BF16, name="a1")
+        att_p = keep.tile([P, P], F32, name="att_p")
         g0 = keep.tile([P, P], BF16, name="g0")
         g1 = keep.tile([P, P], BF16, name="g1")
         gb = keep.tile([P, 6], F32, name="gb")
-        eps_t = keep.tile([P, 1], F32, name="eps_t")
+        eps4 = keep.tile([P, 1], F32, name="eps4")
         warm = keep.tile([P, 1], F32, name="warm")
 
-        nc.vector.memset(eps_t[:], EPS)
-        nc.scalar.activation(out=warm[:], in_=eps_t[:], func=ACT.Abs_reciprocal_sqrt)
+        nc.vector.memset(a0[:], 0.0)
         nc.vector.memset(g0[:], 0.0)
-        nc.scalar.dma_start(out=a0[:], in_=h_att[1:3].rearrange("a b o h w -> (a b o h) w"))
+        nc.vector.memset(eps4[:], EPS / 4.0)
+        nc.sync.dma_start(out=a0[0:64, :], in_=h_att[1:3].rearrange("a b o (hh r) w -> (a b o hh) (r w)", r=2))
         nc.scalar.dma_start(out=g0[0:2, :], in_=gamma_u.rearrange("(r c) -> r c", c=P))
         nc.scalar.dma_start(out=g0[2:3, :], in_=gamma_l.rearrange("(r c) -> r c", c=P))
         nc.scalar.dma_start(out=g0[3:5, :], in_=beta_u.rearrange("(r c) -> r c", c=P))
         nc.scalar.dma_start(out=g0[5:6, :], in_=beta_l.rearrange("(r c) -> r c", c=P))
+        nc.scalar.activation(out=warm[:], in_=eps4[:], func=ACT.Abs_reciprocal_sqrt)
 
-        def load_x(i):
+        def load_x(i, parts):
             s, g = divmod(i, 2)
             b, h = divmod(s, 2)
             rows = xp[b, 512 * g : 512 * g + 512].rearrange("(p j) h w -> p j (h w)", j=4)
-            nc.sync.dma_start(out=xr[i][:], in_=rows[:, :, 512 * h : 512 * h + 512])
+            n = 512 // parts
+            for c in range(parts):
+                nc.sync.dma_start(
+                    out=xr[i][:, :, n * c : n * c + n], in_=rows[:, :, 512 * h + n * c : 512 * h + n * c + n]
+                )
 
         def load_w(t):
             for jj in range(2):
@@ -87,31 +97,25 @@ def tile_gnn_kernel(tc, p_nodes, h_nodes, f_nodes, xp, h_att, Wu, Wl, gamma_u, b
             for jj in range(2):
                 nc.sync.dma_start(out=pn[t][jj:P:2, :, :], in_=p_nodes[1 + 2 * t + jj].rearrange("b c h w -> c b (h w)"))
 
-        for i in range(3):
-            load_x(i)
+        load_x(0, 2)
+        for i in range(1, 4):
+            load_x(i, 1)
         for t in range(3):
             load_w(t)
-        for i in range(3, 8):
-            load_x(i)
+        for i in range(4, 8):
+            load_x(i, 1)
         load_p(0)
         load_p(1)
         nc.sync.dma_start(out=h0[:], in_=h_nodes[0].rearrange("b c h w -> (b c) (h w)"))
         nc.sync.dma_start(out=p0[:], in_=p_nodes[0].rearrange("b c h w -> (b c) (h w)"))
         load_p(2)
 
-        make_identity(nc, ident_b[:])
         make_identity(nc, ident_f[:])
-        nc.vector.tensor_copy(out=a1[:], in_=a0[:].unsqueeze(2).to_broadcast([P, 32, 4]))
-        att_t = ps_att.tile([P, 1024], BF16, name="att_t", tag="att")
-        nc.tensor.transpose(att_t[:, 0:P], a1[:].rearrange("p w j -> p (w j)"), ident_b[:])
+        make_identity(nc, ident_b[:])
+        nc.vector.tensor_copy(out=a1[:], in_=a0[:].unsqueeze(2).to_broadcast([P, 64, 4]))
+        att_t = ps_att.tile([P, 512], F32, name="att_t", tag="att")
+        nc.tensor.transpose(att_t[:, 0:P], a1[:].rearrange("p w j -> p (w j)").bitcast(F32), ident_f[:])
         nc.vector.tensor_copy(out=att_p[:], in_=att_t[:, 0:P])
-        nc.vector.tensor_copy(
-            out=g1[:].rearrange("r (c jj) -> r c jj", jj=2), in_=g0[:].rearrange("r (jj c) -> r c jj", jj=2)
-        )
-        g_t = ps_att.tile([P, 1024], BF16, name="g_t", tag="att")
-        nc.tensor.transpose(g_t[:, 0:P], g1[:], ident_b[:])
-        nc.vector.tensor_scalar(out=gb[:], in0=g_t[:, 0:6], scalar1=0.5, scalar2=None, op0=ALU.mult)
-        nc.vector.tensor_scalar(out=half_i[:], in0=ident_f[:], scalar1=0.5, scalar2=None, op0=ALU.mult)
 
         halves = [(a, s, g) for a in range(2) for s in range(4) for g in range(2)]
         att_bank = {}
@@ -121,25 +125,39 @@ def tile_gnn_kernel(tc, p_nodes, h_nodes, f_nodes, xp, h_att, Wu, Wl, gamma_u, b
         def o_tiles(a):
             return (0, 1) if a == 0 else (2,)
 
-        def regroup(engine_copy, u):
-            i, q = divmod(u, 2)
-            dst = xg[i][:, 256 * q : 256 * q + 256, :].rearrange("p (c i) t -> p c t i", i=4)
-            src = xr[i][:, :, 256 * q : 256 * q + 256].rearrange("p t (c i) -> p c t i", i=4)
+        def regroup_runs(engine_copy, i, lo, n):
+            dst = xg[i][:, lo : lo + n, :].rearrange("p (c i) t -> p c t i", i=4)
+            src = xr[i][:, :, lo : lo + n].rearrange("p t (c i) -> p c t i", i=4)
             engine_copy(out=dst, in_=src)
 
-        def scalar_units(i):
-            if i < 8:
+        def gpsimd_share(i):
+            nc.gpsimd.tensor_scalar(
+                out=xg[i][:, 0:G_PIX, :],
+                in0=xr[i][:, :, 0:G_PIX].rearrange("p t w -> p w t"),
+                scalar1=1.0,
+                scalar2=0.0,
+                op0=ALU.mult,
+                op1=ALU.add,
+            )
+
+        def scalar_share(i):
+            if i >= 8:
+                return
+            if G_PIX > 0:
+                if 2 * i not in V_UNITS:
+                    regroup_runs(nc.scalar.copy, i, G_PIX, 512 - G_PIX)
+            else:
                 for q in range(2):
                     if 2 * i + q not in V_UNITS:
-                        regroup(nc.scalar.copy, 2 * i + q)
+                        regroup_runs(nc.scalar.copy, i, 256 * q, 256)
 
         def spread_att(a, s):
             for q in range(2):
-                bank = ps_att.tile([P, 1024], BF16, name="att_bank", tag="att")
-                for r in range(8):
-                    row = 64 * a + 16 * s + 8 * q + r
+                bank = ps_att.tile([P, 512], F32, name="att_bank", tag="att")
+                for r in range(4):
+                    row = 32 * a + 8 * s + 4 * q + r
                     nc.tensor.transpose(
-                        bank[:, P * r : P * r + P], att_p[:, row : row + 1].to_broadcast([P, P]), ident_b[:]
+                        bank[:, P * r : P * r + P], att_p[:, row : row + 1].to_broadcast([P, P]), ident_f[:]
                     )
                 att_bank[(a, s, q)] = bank
 
@@ -150,12 +168,24 @@ def tile_gnn_kernel(tc, p_nodes, h_nodes, f_nodes, xp, h_att, Wu, Wl, gamma_u, b
             nc.vector.tensor_tensor(
                 out=prod[k][:, 1024 * q : 1024 * q + 1024],
                 in0=xg[2 * s + g][:, 256 * q : 256 * q + 256, :].rearrange("p w j -> p (w j)"),
-                in1=att_bank[(a, s, q)][:],
+                in1=att_bank[(a, s, q)][:].bitcast(BF16),
                 op=ALU.mult,
             )
 
         def quantise(k):
             nc.vector.quantize_mx(out=xc[k][:].bitcast(FP8X4), scales=xs[k][:], in_=prod[k][:])
+
+        def gains():
+            nc.vector.tensor_copy(
+                out=g1[:].rearrange("r (c jj) -> r c jj", jj=2), in_=g0[:].rearrange("r (jj c) -> r c jj", jj=2)
+            )
+            g_t = ps_y.tile([P, 1024], BF16, name="g_t", tag="y")
+            nc.tensor.transpose(g_t[:, 0:P], g1[:], ident_b[:])
+            y_bank["g"] = g_t
+
+        def gains_out():
+            nc.vector.tensor_scalar(out=gb[:], in0=y_bank["g"][:, 0:6], scalar1=0.5, scalar2=None, op0=ALU.mult)
+            nc.vector.tensor_scalar(out=half_i[:], in0=ident_f[:], scalar1=0.5, scalar2=None, op0=ALU.mult)
 
         def w_transpose(t):
             bank = ps_y.tile([P, 512], F32, name="w_bank", tag="y")
@@ -195,23 +225,33 @@ def tile_gnn_kernel(tc, p_nodes, h_nodes, f_nodes, xp, h_att, Wu, Wl, gamma_u, b
                 y_bank[(t, s)] = bank
 
         def take_out(a, s):
+            cols = slice(512 * s, 512 * s + 512)
             for t in o_tiles(a):
                 nc.scalar.activation(
-                    out=y_sb[t][:, 512 * s : 512 * s + 512],
+                    out=y_sb[t][:, cols], in_=y_bank[(t, s)][:], func=ACT.Identity, accum_out=sums[t][:, s : s + 1]
+                )
+            if s == 0:
+                for t in o_tiles(a):
+                    nc.scalar.activation(out=negc[t][:], in_=sums[t][:, 0:1], func=ACT.Identity, scale=-1.0 / 512.0)
+            for t in o_tiles(a):
+                nc.scalar.activation(
+                    out=o_sb[t][:, cols],
                     in_=y_bank[(t, s)][:],
-                    func=ACT.Identity,
-                    accum_out=sums[t][:, s : s + 1],
+                    func=ACT.Square,
+                    bias=negc[t][:],
+                    accum_out=sqs[t][:, s : s + 1],
                 )
 
         def statistics(t):
             nc.scalar.activation(
-                out=junk4[t][:], in_=sums[t][:], func=ACT.Identity, scale=-1.0 / NPIX, accum_out=negmean[t][:]
+                out=junk_a[t][:], in_=sums[t][:], func=ACT.Identity, scale=-1.0 / NPIX, accum_out=negmean[t][:]
             )
             nc.scalar.activation(
-                out=o_sb[t][:], in_=y_sb[t][:], func=ACT.Square, bias=negmean[t][:], accum_out=m2[t][:]
+                out=junk_b[t][:], in_=sqs[t][:], func=ACT.Identity, scale=1.0 / NPIX, bias=eps4[:], accum_out=msq[t][:]
             )
+            nc.scalar.activation(out=dsq[t][:], in_=negc[t][:], func=ACT.Square, scale=-1.0, bias=negmean[t][:])
             nc.scalar.activation(
-                out=rstd[t][:], in_=m2[t][:], func=ACT.Abs_reciprocal_sqrt, scale=1.0 / NPIX, bias=eps_t[:]
+                out=rstd[t][:], in_=dsq[t][:], func=ACT.Abs_reciprocal_sqrt, scale=-1.0, bias=msq[t][:]
             )
             nc.scalar.activation(out=scl[t][:], in_=gb[:, t : t + 1], func=ACT.Identity, scale=rstd[t][:])
             nc.scalar.activation(
@@ -249,7 +289,11 @@ def tile_gnn_kernel(tc, p_nodes, h_nodes, f_nodes, xp, h_att, Wu, Wl, gamma_u, b
             nc.scalar.copy(out=o0[:, 512 * h : 512 * h + 512], in_=y_bank[("o0", h)][:])
 
         def fill(k):
+            if k == 0:
+                gains()
             if k == 1:
+                gains_out()
+            if k == 2:
                 for t in range(3):
                     w_transpose(t)
                 for t in range(3):
@@ -259,41 +303,48 @@ def tile_gnn_kernel(tc, p_nodes, h_nodes, f_nodes, xp, h_att, Wu, Wl, gamma_u, b
                     w_quantise(t)
             if k == 5:
                 take_out(0, 0)
-            if k == 7:
+            if k == 6:
                 take_out(0, 1)
-            if k == 9:
+            if k == 7:
                 take_out(0, 2)
-            if k == 10:
+            if k == 9:
                 take_out(0, 3)
                 statistics(0)
-            if k == 11:
                 statistics(1)
+            if k == 10:
+                relu(0, 0, 1024)
+            if k == 11:
+                take_out(1, 0)
+                relu(0, 1024, 1024)
             if k == 12:
                 node0_sum(0)
                 node0_sum(1)
-                take_out(1, 0)
-                relu(0, 0, 1024)
-                relu(0, 1024, 1024)
+                relu(1, 0, 1024)
             if k == 13:
+                take_out(1, 1)
                 node0_out(0)
                 node0_out(1)
                 nc.sync.dma_start(out=out[0].rearrange("b c h w -> (b c) (h w)"), in_=o0[:])
-                relu(1, 0, 1024)
             if k == 14:
-                take_out(1, 1)
                 relu(1, 1024, 1024)
+            if k == 15:
+                take_out(1, 2)
 
         spread_att(0, 0)
+        if G_PIX > 0:
+            for i in range(8):
+                if 2 * i not in V_UNITS:
+                    gpsimd_share(i)
         for i in range(LOOKAHEAD):
-            scalar_units(i)
+            scalar_share(i)
         for k in range(16):
             a, s, g = halves[k]
-            scalar_units(k + LOOKAHEAD)
+            scalar_share(k + LOOKAHEAD)
             if g == 0 and k + 2 < 16:
                 spread_att(halves[k + 2][0], halves[k + 2][1])
             for q in range(2):
                 if a == 0 and 2 * k + q in V_UNITS:
-                    regroup(nc.vector.tensor_copy, 2 * k + q)
+                    regroup_runs(nc.vector.tensor_copy, k, 256 * q, 256)
                 if q == 1 and k > 0:
                     quantise(k - 1)
                 multiply(k, q)
@@ -304,7 +355,6 @@ def tile_gnn_kernel(tc, p_nodes, h_nodes, f_nodes, xp, h_att, Wu, Wl, gamma_u, b
             fill(k)
         quantise(15)
         convolve(1, 3)
-        take_out(1, 2)
         take_out(1, 3)
         statistics(2)
         for t in range(2):

@@ -17,8 +17,8 @@ ALU = mybir.AluOpType
 P = 128
 EPS = 1e-5
 NPIX = 2048
-V_UNITS = (0, 1, 4, 8, 11, 14)
-G_PIX = 0
+V_UNITS = (0, 1)
+G_PIX = 192
 LOOKAHEAD = 2
 
 

@@ -27,8 +27,8 @@ def tile_gnn_kernel(tc, p_nodes, h_nodes, f_nodes, xp, h_att, Wu, Wl, gamma_u, b
     with ExitStack() as ctx:
         keep = ctx.enter_context(tc.tile_pool(name="keep", bufs=1))
         prods = ctx.enter_context(tc.tile_pool(name="prods", bufs=3))
-        ps_att = ctx.enter_context(tc.psum_pool(name="ps_att", bufs=4))
-        ps_y = ctx.enter_context(tc.psum_pool(name="ps_y", bufs=4))
+        ps_att = ctx.enter_context(tc.psum_pool(name="ps_att", bufs=3))
+        ps_y = ctx.enter_context(tc.psum_pool(name="ps_y", bufs=5))
         ctx.enter_context(tc.manual_schedule())
 
         xr = [keep.tile([P, 4, 512], BF16, name="xr%d" % i) for i in range(8)]
@@ -59,8 +59,8 @@ def tile_gnn_kernel(tc, p_nodes, h_nodes, f_nodes, xp, h_att, Wu, Wl, gamma_u, b
         ident_f = keep.tile([P, P], F32, name="ident_f")
         ident_b = keep.tile([P, P], BF16, name="ident_b")
         half_i = keep.tile([P, P], BF16, name="half_i")
-        a0 = keep.tile([P, 64], BF16, name="a0")
-        a1 = keep.tile([P, 64, 4], BF16, name="a1")
+        a0 = keep.tile([P, P], BF16, name="a0")
+        a1 = keep.tile([P, P, 2], BF16, name="a1")
         att_p = keep.tile([P, P], F32, name="att_p")
         g0 = keep.tile([P, P], BF16, name="g0")
         g1 = keep.tile([P, P], BF16, name="g1")
@@ -71,7 +71,7 @@ def tile_gnn_kernel(tc, p_nodes, h_nodes, f_nodes, xp, h_att, Wu, Wl, gamma_u, b
         nc.vector.memset(a0[:], 0.0)
         nc.vector.memset(g0[:], 0.0)
         nc.vector.memset(eps4[:], EPS / 4.0)
-        nc.sync.dma_start(out=a0[0:64, :], in_=h_att[1:3].rearrange("a b o (hh r) w -> (a b o hh) (r w)", r=2))
+        nc.sync.dma_start(out=a0[0:32, :], in_=h_att[1:3].rearrange("a b o (hh r) w -> (a b o hh) (r w)", r=4))
         nc.scalar.dma_start(out=g0[0:2, :], in_=gamma_u.rearrange("(r c) -> r c", c=P))
         nc.scalar.dma_start(out=g0[2:3, :], in_=gamma_l.rearrange("(r c) -> r c", c=P))
         nc.scalar.dma_start(out=g0[3:5, :], in_=beta_u.rearrange("(r c) -> r c", c=P))
@@ -112,7 +112,7 @@ def tile_gnn_kernel(tc, p_nodes, h_nodes, f_nodes, xp, h_att, Wu, Wl, gamma_u, b
 
         make_identity(nc, ident_f[:])
         make_identity(nc, ident_b[:])
-        nc.vector.tensor_copy(out=a1[:], in_=a0[:].unsqueeze(2).to_broadcast([P, 64, 4]))
+        nc.vector.tensor_copy(out=a1[:], in_=a0[:].unsqueeze(2).to_broadcast([P, P, 2]))
         att_t = ps_att.tile([P, 512], F32, name="att_t", tag="att")
         nc.tensor.transpose(att_t[:, 0:P], a1[:].rearrange("p w j -> p (w j)").bitcast(F32), ident_f[:])
         nc.vector.tensor_copy(out=att_p[:], in_=att_t[:, 0:P])
@@ -152,23 +152,26 @@ def tile_gnn_kernel(tc, p_nodes, h_nodes, f_nodes, xp, h_att, Wu, Wl, gamma_u, b
                         regroup_runs(nc.scalar.copy, i, 256 * q, 256)
 
         def spread_att(a, s):
-            for q in range(2):
-                bank = ps_att.tile([P, 512], F32, name="att_bank", tag="att")
-                for r in range(4):
-                    row = 32 * a + 8 * s + 4 * q + r
-                    nc.tensor.transpose(
-                        bank[:, P * r : P * r + P], att_p[:, row : row + 1].to_broadcast([P, P]), ident_f[:]
-                    )
-                att_bank[(a, s, q)] = bank
+            bank = ps_att.tile([P, 512], F32, name="att_bank", tag="att")
+            for r in range(4):
+                row = 16 * a + 4 * s + r
+                nc.tensor.transpose(
+                    bank[:, P * r : P * r + P], att_p[:, row : row + 1].to_broadcast([P, P]), ident_f[:]
+                )
+            att_bank[(a, s)] = bank
 
-        def multiply(k, q):
+        def multiply(k, lo, n):
             a, s, g = halves[k]
-            if q == 0:
+            if lo == 0:
                 prod[k] = prods.tile([P, 2048], BF16, name="prod", tag="prod", align_bytes=64)
             nc.vector.tensor_tensor(
-                out=prod[k][:, 1024 * q : 1024 * q + 1024],
-                in0=xg[2 * s + g][:, 256 * q : 256 * q + 256, :].rearrange("p w j -> p (w j)"),
-                in1=att_bank[(a, s, q)][:].bitcast(BF16),
+                out=prod[k][:, 4 * lo : 4 * (lo + n)].rearrange("p (w u e) -> p w u e", u=2, e=2),
+                in0=xg[2 * s + g][:, lo : lo + n, :].rearrange("p w (u e) -> p w u e", e=2),
+                in1=att_bank[(a, s)][:, lo : lo + n]
+                .bitcast(BF16)
+                .rearrange("p (w e) -> p w e", e=2)
+                .unsqueeze(2)
+                .to_broadcast([P, n, 2, 2]),
                 op=ALU.mult,
             )
 
@@ -342,12 +345,13 @@ def tile_gnn_kernel(tc, p_nodes, h_nodes, f_nodes, xp, h_att, Wu, Wl, gamma_u, b
             scalar_share(k + LOOKAHEAD)
             if g == 0 and k + 2 < 16:
                 spread_att(halves[k + 2][0], halves[k + 2][1])
-            for q in range(2):
-                if a == 0 and 2 * k + q in V_UNITS:
+            if k == 0:
+                for q in range(2):
                     regroup_runs(nc.vector.tensor_copy, k, 256 * q, 256)
-                if q == 1 and k > 0:
-                    quantise(k - 1)
-                multiply(k, q)
+                    multiply(k, 256 * q, 256)
+            else:
+                multiply(k, 0, 512)
+                quantise(k - 1)
             if k == 4:
                 convolve(0, 0)
             if g == 0 and k >= 4:

@@ -28,7 +28,8 @@ def tile_gnn_kernel(tc, p_nodes, h_nodes, f_nodes, xp, h_att, Wu, Wl, gamma_u, b
         keep = ctx.enter_context(tc.tile_pool(name="keep", bufs=1))
         prods = ctx.enter_context(tc.tile_pool(name="prods", bufs=3))
         ps_att = ctx.enter_context(tc.psum_pool(name="ps_att", bufs=3))
-        ps_y = ctx.enter_context(tc.psum_pool(name="ps_y", bufs=5))
+        ps_y = ctx.enter_context(tc.psum_pool(name="ps_y", bufs=4))
+        ps_acc = ctx.enter_context(tc.psum_pool(name="ps_acc", bufs=1))
         ctx.enter_context(tc.manual_schedule())
 
         xr = [keep.tile([P, 4, 512], BF16, name="xr%d" % i) for i in range(8)]
@@ -36,9 +37,11 @@ def tile_gnn_kernel(tc, p_nodes, h_nodes, f_nodes, xp, h_att, Wu, Wl, gamma_u, b
         xc = [keep.tile([P, 512], U32, name="xc%d" % k, align_bytes=64) for k in range(16)]
         xs = [keep.tile([P, 512], U8, name="xs%d" % k, align_bytes=64) for k in range(16)]
         w_sb = [keep.tile([P, 1024], BF16, name="w_sb%d" % t) for t in range(3)]
-        wg = [keep.tile([P, 1024], BF16, name="wg%d" % t, align_bytes=64) for t in range(3)]
-        wc = [keep.tile([P, 256], U32, name="wc%d" % t, align_bytes=64) for t in range(3)]
-        ws = [keep.tile([P, 256], U8, name="ws%d" % t, align_bytes=64) for t in range(3)]
+        wg = keep.tile([P, 2, 3, 512], BF16, name="wg", align_bytes=64)
+        wc = keep.tile([P, 768], U32, name="wc", align_bytes=64)
+        ws = keep.tile([P, 768], U8, name="ws", align_bytes=64)
+        acc_sb = keep.tile([P, 256], F32, name="acc_sb")
+        ones = keep.tile([P, 1], F32, name="ones")
         y_sb = [keep.tile([P, NPIX], F32, name="y_sb%d" % t) for t in range(3)]
         o_sb = [keep.tile([P, NPIX], F32, name="o_sb%d" % t) for t in range(3)]
         pn = [keep.tile([P, 2, 1024], BF16, name="pn%d" % t) for t in range(3)]
@@ -71,6 +74,7 @@ def tile_gnn_kernel(tc, p_nodes, h_nodes, f_nodes, xp, h_att, Wu, Wl, gamma_u, b
         nc.vector.memset(a0[:], 0.0)
         nc.vector.memset(g0[:], 0.0)
         nc.vector.memset(eps4[:], EPS / 4.0)
+        nc.vector.memset(ones[:], 1.0)
         nc.sync.dma_start(out=a0[0:32, :], in_=h_att[1:3].rearrange("a b o (hh r) w -> (a b o hh) (r w)", r=4))
         nc.scalar.dma_start(out=g0[0:2, :], in_=gamma_u.rearrange("(r c) -> r c", c=P))
         nc.scalar.dma_start(out=g0[2:3, :], in_=gamma_l.rearrange("(r c) -> r c", c=P))
@@ -204,28 +208,89 @@ def tile_gnn_kernel(tc, p_nodes, h_nodes, f_nodes, xp, h_att, Wu, Wl, gamma_u, b
 
         def w_copy(t):
             nc.scalar.copy(
-                out=wg[t][:].bitcast(F32).rearrange("p (g o u) -> p g o u", g=2, u=2),
+                out=wg[:, :, t, :].bitcast(F32).rearrange("p g (o u) -> p g o u", u=2),
                 in_=y_bank[("w", t)][:].rearrange("p (g u o) -> p g o u", g=2, u=2),
             )
 
         def w_quantise(t):
-            nc.vector.quantize_mx(out=wc[t][:].bitcast(FP8X4), scales=ws[t][:], in_=wg[t][:])
+            nc.vector.quantize_mx(
+                out=wc[:, 256 * t : 256 * t + 256].bitcast(FP8X4),
+                scales=ws[:, 256 * t : 256 * t + 256],
+                in_=wg[:].rearrange("p g t c -> p (g t c)")[:, 1024 * t : 1024 * t + 1024],
+            )
+
+        def convolve_tile(t, a, s):
+            bank = ps_y.tile([P, 512], F32, name="y_bank", tag="y")
+            for g in range(2):
+                k = 8 * a + 2 * s + g
+                w0 = 384 * g + P * t
+                nc.tensor.matmul_mx(
+                    out=bank[:],
+                    lhsT=wc[:, w0 : w0 + P].bitcast(FP8X4),
+                    lhsT_scale=ws[:, w0 : w0 + P],
+                    rhs=xc[k][:].bitcast(FP8X4),
+                    rhs_scale=xs[k][:],
+                    start=(g == 0),
+                    stop=(g == 1),
+                )
+            y_bank[(t, s)] = bank
+
+        def sum_pixels(s):
+            for g in range(2):
+                k = 2 * s + g
+                for m in range(4):
+                    nc.tensor.matmul_mx(
+                        out=acc[:, 0:256],
+                        lhsT=xc[k][:, P * m : P * m + P].bitcast(FP8X4),
+                        lhsT_scale=xs[k][:, P * m : P * m + P],
+                        rhs=wc[:, 384 * g : 384 * g + 256].bitcast(FP8X4),
+                        rhs_scale=ws[:, 384 * g : 384 * g + 256],
+                        start=(s == 0 and g == 0 and m == 0),
+                        stop=(s == 3 and g == 1 and m == 3),
+                    )
 
         def convolve(a, s):
             for t in o_tiles(a):
-                bank = ps_y.tile([P, 512], F32, name="y_bank", tag="y")
-                for g in range(2):
-                    k = 8 * a + 2 * s + g
-                    nc.tensor.matmul_mx(
-                        out=bank[:],
-                        lhsT=wc[t][:, P * g : P * g + P].bitcast(FP8X4),
-                        lhsT_scale=ws[t][:, P * g : P * g + P],
-                        rhs=xc[k][:].bitcast(FP8X4),
-                        rhs_scale=xs[k][:],
-                        start=(g == 0),
-                        stop=(g == 1),
+                convolve_tile(t, a, s)
+            if a == 0:
+                sum_pixels(s)
+
+        def upper_squares(s):
+            cols = slice(512 * s, 512 * s + 512)
+            if s == 0:
+                for t in range(2):
+                    nc.scalar.activation(
+                        out=y_sb[t][:, cols], in_=y_bank[(t, s)][:], func=ACT.Identity, accum_out=sums[t][:, 0:1]
                     )
-                y_bank[(t, s)] = bank
+                for t in range(2):
+                    nc.scalar.activation(out=negc[t][:], in_=sums[t][:, 0:1], func=ACT.Identity, scale=-1.0 / 512.0)
+            for t in range(2):
+                nc.scalar.activation(
+                    out=o_sb[t][:, cols],
+                    in_=y_bank[(t, s)][:],
+                    func=ACT.Square,
+                    bias=negc[t][:],
+                    accum_out=sqs[t][:, s : s + 1],
+                )
+
+        def upper_means():
+            nc.scalar.copy(out=acc_sb[:], in_=acc[:, 0:256])
+            bank = ps_y.tile([P, 512], F32, name="mean_bank", tag="y")
+            for t in range(2):
+                nc.tensor.matmul(
+                    out=bank[:, t : t + 1], lhsT=acc_sb[:, P * t : P * t + P], rhs=ones[:], start=True, stop=True
+                )
+            for t in range(2):
+                nc.scalar.activation(out=negmean[t][:], in_=bank[:, t : t + 1], func=ACT.Identity, scale=-1.0 / NPIX)
+
+        def relu_bank(t, s):
+            nc.scalar.activation(
+                out=y_sb[t][:, 512 * s : 512 * s + 512],
+                in_=y_bank[(t, s)][:],
+                func=ACT.Relu,
+                scale=scl[t][:],
+                bias=bia[t][:],
+            )
 
         def take_out(a, s):
             cols = slice(512 * s, 512 * s + 512)
@@ -246,9 +311,10 @@ def tile_gnn_kernel(tc, p_nodes, h_nodes, f_nodes, xp, h_att, Wu, Wl, gamma_u, b
                 )
 
         def statistics(t):
-            nc.scalar.activation(
-                out=junk_a[t][:], in_=sums[t][:], func=ACT.Identity, scale=-1.0 / NPIX, accum_out=negmean[t][:]
-            )
+            if t == 2:
+                nc.scalar.activation(
+                    out=junk_a[t][:], in_=sums[t][:], func=ACT.Identity, scale=-1.0 / NPIX, accum_out=negmean[t][:]
+                )
             nc.scalar.activation(
                 out=junk_b[t][:], in_=sqs[t][:], func=ACT.Identity, scale=1.0 / NPIX, bias=eps4[:], accum_out=msq[t][:]
             )
@@ -305,35 +371,50 @@ def tile_gnn_kernel(tc, p_nodes, h_nodes, f_nodes, xp, h_att, Wu, Wl, gamma_u, b
                 for t in range(3):
                     w_quantise(t)
             if k == 5:
-                take_out(0, 0)
+                upper_squares(0)
             if k == 6:
-                take_out(0, 1)
+                upper_squares(1)
             if k == 7:
-                take_out(0, 2)
+                upper_squares(2)
             if k == 9:
-                take_out(0, 3)
+                upper_squares(3)
+                upper_means()
                 statistics(0)
                 statistics(1)
+                convolve_tile(0, 0, 0)
+                convolve_tile(0, 0, 1)
             if k == 10:
-                relu(0, 0, 1024)
+                relu_bank(0, 0)
+                relu_bank(0, 1)
+                convolve_tile(0, 0, 2)
+                convolve_tile(0, 0, 3)
             if k == 11:
                 take_out(1, 0)
-                relu(0, 1024, 1024)
+                relu_bank(0, 2)
+                relu_bank(0, 3)
+                convolve_tile(1, 0, 0)
+                convolve_tile(1, 0, 1)
             if k == 12:
+                relu_bank(1, 0)
+                relu_bank(1, 1)
                 node0_sum(0)
                 node0_sum(1)
-                relu(1, 0, 1024)
             if k == 13:
                 take_out(1, 1)
                 node0_out(0)
                 node0_out(1)
                 nc.sync.dma_start(out=out[0].rearrange("b c h w -> (b c) (h w)"), in_=o0[:])
+                convolve_tile(1, 0, 2)
+                convolve_tile(1, 0, 3)
             if k == 14:
-                relu(1, 1024, 1024)
+                relu_bank(1, 2)
+                relu_bank(1, 3)
             if k == 15:
                 take_out(1, 2)
 
+        acc = ps_acc.tile([P, 512], F32, name="acc")
         spread_att(0, 0)
+        spread_att(0, 1)
         if G_PIX > 0:
             for i in range(8):
                 if 2 * i not in V_UNITS:
@@ -343,8 +424,8 @@ def tile_gnn_kernel(tc, p_nodes, h_nodes, f_nodes, xp, h_att, Wu, Wl, gamma_u, b
         for k in range(16):
             a, s, g = halves[k]
             scalar_share(k + LOOKAHEAD)
-            if g == 0 and k + 2 < 16:
-                spread_att(halves[k + 2][0], halves[k + 2][1])
+            if g == 0 and k + 4 < 16:
+                spread_att(halves[k + 4][0], halves[k + 4][1])
             if k == 0:
                 for q in range(2):
                     regroup_runs(nc.vector.tensor_copy, k, 256 * q, 256)

@@ -71,7 +71,8 @@ def tile_gnn_kernel(tc, p_nodes, h_nodes, f_nodes, xp, h_att, Wu, Wl, gamma_u, b
         eps4 = keep.tile([P, 1], F32, name="eps4")
         warm = keep.tile([P, 1], F32, name="warm")
 
-        nc.vector.memset(a0[:], 0.0)
+        nc.vector.memset(a0[32:64, :], 0.0)
+        nc.vector.memset(a0[64:P, :], 0.0)
         nc.vector.memset(g0[:], 0.0)
         nc.vector.memset(eps4[:], EPS / 4.0)
         nc.vector.memset(ones[:], 1.0)
@@ -119,7 +120,7 @@ def tile_gnn_kernel(tc, p_nodes, h_nodes, f_nodes, xp, h_att, Wu, Wl, gamma_u, b
         nc.vector.tensor_copy(out=a1[:], in_=a0[:].unsqueeze(2).to_broadcast([P, P, 2]))
         att_t = ps_att.tile([P, 512], F32, name="att_t", tag="att")
         nc.tensor.transpose(att_t[:, 0:P], a1[:].rearrange("p w j -> p (w j)").bitcast(F32), ident_f[:])
-        nc.vector.tensor_copy(out=att_p[:], in_=att_t[:, 0:P])
+        nc.scalar.copy(out=att_p[:], in_=att_t[:, 0:P])
 
         halves = [(a, s, g) for a in range(2) for s in range(4) for g in range(2)]
         att_bank = {}
@@ -429,7 +430,7 @@ def tile_gnn_kernel(tc, p_nodes, h_nodes, f_nodes, xp, h_att, Wu, Wl, gamma_u, b
             if k == 0:
                 for q in range(2):
                     regroup_runs(nc.vector.tensor_copy, k, 256 * q, 256)
-                    multiply(k, 256 * q, 256)
+                multiply(k, 0, 512)
             else:
                 multiply(k, 0, 512)
                 quantise(k - 1)

@@ -251,9 +251,11 @@ def tile_gnn_kernel(tc, p_nodes, h_nodes, f_nodes, xp, h_att, Wu, Wl, gamma_u, b
                     )
 
         def convolve(a, s):
+            if a == 0 and s == 3:
+                sum_pixels(s)
             for t in o_tiles(a):
                 convolve_tile(t, a, s)
-            if a == 0:
+            if a == 0 and s < 3:
                 sum_pixels(s)
 
         def upper_squares(s):
@@ -281,8 +283,13 @@ def tile_gnn_kernel(tc, p_nodes, h_nodes, f_nodes, xp, h_att, Wu, Wl, gamma_u, b
                 nc.tensor.matmul(
                     out=bank[:, t : t + 1], lhsT=acc_sb[:, P * t : P * t + P], rhs=ones[:], start=True, stop=True
                 )
+            y_bank["mean"] = bank
+
+        def upper_means_out():
             for t in range(2):
-                nc.scalar.activation(out=negmean[t][:], in_=bank[:, t : t + 1], func=ACT.Identity, scale=-1.0 / NPIX)
+                nc.scalar.activation(
+                    out=negmean[t][:], in_=y_bank["mean"][:, t : t + 1], func=ACT.Identity, scale=-1.0 / NPIX
+                )
 
         def relu_bank(t, s):
             nc.scalar.activation(
@@ -299,6 +306,11 @@ def tile_gnn_kernel(tc, p_nodes, h_nodes, f_nodes, xp, h_att, Wu, Wl, gamma_u, b
                 nc.scalar.activation(
                     out=y_sb[t][:, cols], in_=y_bank[(t, s)][:], func=ACT.Identity, accum_out=sums[t][:, s : s + 1]
                 )
+            if s == 3:
+                for t in o_tiles(a):
+                    nc.scalar.activation(
+                        out=junk_a[t][:], in_=sums[t][:], func=ACT.Identity, scale=-1.0 / NPIX, accum_out=negmean[t][:]
+                    )
             if s == 0:
                 for t in o_tiles(a):
                     nc.scalar.activation(out=negc[t][:], in_=sums[t][:, 0:1], func=ACT.Identity, scale=-1.0 / 512.0)
@@ -311,22 +323,28 @@ def tile_gnn_kernel(tc, p_nodes, h_nodes, f_nodes, xp, h_att, Wu, Wl, gamma_u, b
                     accum_out=sqs[t][:, s : s + 1],
                 )
 
-        def statistics(t):
-            if t == 2:
+        def statistics(tiles):
+            for t in tiles:
+                nc.scalar.activation(out=dsq[t][:], in_=negc[t][:], func=ACT.Square, scale=-1.0, bias=negmean[t][:])
+            for t in tiles:
                 nc.scalar.activation(
-                    out=junk_a[t][:], in_=sums[t][:], func=ACT.Identity, scale=-1.0 / NPIX, accum_out=negmean[t][:]
+                    out=junk_b[t][:],
+                    in_=sqs[t][:],
+                    func=ACT.Identity,
+                    scale=1.0 / NPIX,
+                    bias=eps4[:],
+                    accum_out=msq[t][:],
                 )
-            nc.scalar.activation(
-                out=junk_b[t][:], in_=sqs[t][:], func=ACT.Identity, scale=1.0 / NPIX, bias=eps4[:], accum_out=msq[t][:]
-            )
-            nc.scalar.activation(out=dsq[t][:], in_=negc[t][:], func=ACT.Square, scale=-1.0, bias=negmean[t][:])
-            nc.scalar.activation(
-                out=rstd[t][:], in_=dsq[t][:], func=ACT.Abs_reciprocal_sqrt, scale=-1.0, bias=msq[t][:]
-            )
-            nc.scalar.activation(out=scl[t][:], in_=gb[:, t : t + 1], func=ACT.Identity, scale=rstd[t][:])
-            nc.scalar.activation(
-                out=bia[t][:], in_=negmean[t][:], func=ACT.Identity, scale=scl[t][:], bias=gb[:, 3 + t : 4 + t]
-            )
+            for t in tiles:
+                nc.scalar.activation(
+                    out=rstd[t][:], in_=dsq[t][:], func=ACT.Abs_reciprocal_sqrt, scale=-1.0, bias=msq[t][:]
+                )
+            for t in tiles:
+                nc.scalar.activation(out=scl[t][:], in_=gb[:, t : t + 1], func=ACT.Identity, scale=rstd[t][:])
+            for t in tiles:
+                nc.scalar.activation(
+                    out=bia[t][:], in_=negmean[t][:], func=ACT.Identity, scale=scl[t][:], bias=gb[:, 3 + t : 4 + t]
+                )
 
         def relu(t, lo, n):
             nc.scalar.activation(
@@ -378,10 +396,10 @@ def tile_gnn_kernel(tc, p_nodes, h_nodes, f_nodes, xp, h_att, Wu, Wl, gamma_u, b
             if k == 7:
                 upper_squares(2)
             if k == 9:
-                upper_squares(3)
                 upper_means()
-                statistics(0)
-                statistics(1)
+                upper_squares(3)
+                upper_means_out()
+                statistics((0, 1))
                 convolve_tile(0, 0, 0)
                 convolve_tile(0, 0, 1)
             if k == 10:
@@ -442,7 +460,7 @@ def tile_gnn_kernel(tc, p_nodes, h_nodes, f_nodes, xp, h_att, Wu, Wl, gamma_u, b
         quantise(15)
         convolve(1, 3)
         take_out(1, 3)
-        statistics(2)
+        statistics((2,))
         for t in range(2):
             for b in range(2):
                 average(t, 1024 * b, 1024)

@@ -19,7 +19,7 @@ EPS = 1e-5
 NPIX = 2048
 V_UNITS = (0, 1)
 G_PIX = 192
-LOOKAHEAD = 2
+SHIFT_PIX = 64
 
 
 def tile_gnn_kernel(tc, p_nodes, h_nodes, f_nodes, xp, h_att, Wu, Wl, gamma_u, beta_u, gamma_l, beta_l, out):
@@ -115,14 +115,31 @@ def tile_gnn_kernel(tc, p_nodes, h_nodes, f_nodes, xp, h_att, Wu, Wl, gamma_u, b
         nc.sync.dma_start(out=p0[:], in_=p_nodes[0].rearrange("b c h w -> (b c) (h w)"))
         load_p(2)
 
-        make_identity(nc, ident_f[:])
         make_identity(nc, ident_b[:])
-        nc.vector.tensor_copy(out=a1[:], in_=a0[:].unsqueeze(2).to_broadcast([P, P, 2]))
+        make_identity(nc, ident_f[:])
+
+        def spread_rows(a, s):
+            bank = ps_att.tile([P, 1024], BF16, name="row_bank", tag="att")
+            for r in range(4):
+                row = 16 * a + 4 * s + r
+                nc.tensor.matmul(
+                    out=bank[:, 256 * r : 256 * r + 256],
+                    lhsT=ident_b[:, row : row + 1].to_broadcast([P, P]),
+                    rhs=a0[:].unsqueeze(2).to_broadcast([P, P, 2]),
+                    start=True,
+                    stop=True,
+                )
+            return bank[:]
+
+        first_banks = [spread_rows(0, 0), spread_rows(1, 0)]
+        nc.gpsimd.tensor_copy(out=a1[:], in_=a0[:].unsqueeze(2).to_broadcast([P, P, 2]))
         att_t = ps_att.tile([P, 512], F32, name="att_t", tag="att")
         nc.tensor.transpose(att_t[:, 0:P], a1[:].rearrange("p w j -> p (w j)").bitcast(F32), ident_f[:])
         nc.scalar.copy(out=att_p[:], in_=att_t[:, 0:P])
 
-        halves = [(a, s, g) for a in range(2) for s in range(4) for g in range(2)]
+        blocks = [(0, 0), (1, 0), (0, 1), (0, 2), (0, 3), (1, 1), (1, 2), (1, 3)]
+        halves = [(a, 0, g) for g in range(2) for a in range(2)] + [(a, s, g) for a, s in blocks[2:] for g in range(2)]
+        step_of = {half: k for k, half in enumerate(halves)}
         att_bank = {}
         prod = {}
         y_bank = {}
@@ -163,7 +180,7 @@ def tile_gnn_kernel(tc, p_nodes, h_nodes, f_nodes, xp, h_att, Wu, Wl, gamma_u, b
                 nc.tensor.transpose(
                     bank[:, P * r : P * r + P], att_p[:, row : row + 1].to_broadcast([P, P]), ident_f[:]
                 )
-            att_bank[(a, s)] = bank
+            att_bank[(a, s)] = bank[:].bitcast(BF16)
 
         def multiply(k, lo, n):
             a, s, g = halves[k]
@@ -172,8 +189,7 @@ def tile_gnn_kernel(tc, p_nodes, h_nodes, f_nodes, xp, h_att, Wu, Wl, gamma_u, b
             nc.vector.tensor_tensor(
                 out=prod[k][:, 4 * lo : 4 * (lo + n)].rearrange("p (w u e) -> p w u e", u=2, e=2),
                 in0=xg[2 * s + g][:, lo : lo + n, :].rearrange("p w (u e) -> p w u e", e=2),
-                in1=att_bank[(a, s)][:, lo : lo + n]
-                .bitcast(BF16)
+                in1=att_bank[(a, s)][:, 2 * lo : 2 * (lo + n)]
                 .rearrange("p (w e) -> p w e", e=2)
                 .unsqueeze(2)
                 .to_broadcast([P, n, 2, 2]),
@@ -223,7 +239,7 @@ def tile_gnn_kernel(tc, p_nodes, h_nodes, f_nodes, xp, h_att, Wu, Wl, gamma_u, b
         def convolve_tile(t, a, s):
             bank = ps_y.tile([P, 512], F32, name="y_bank", tag="y")
             for g in range(2):
-                k = 8 * a + 2 * s + g
+                k = step_of[(a, s, g)]
                 w0 = 384 * g + P * t
                 nc.tensor.matmul_mx(
                     out=bank[:],
@@ -238,7 +254,7 @@ def tile_gnn_kernel(tc, p_nodes, h_nodes, f_nodes, xp, h_att, Wu, Wl, gamma_u, b
 
         def sum_pixels(s):
             for g in range(2):
-                k = 2 * s + g
+                k = step_of[(0, s, g)]
                 for m in range(4):
                     nc.tensor.matmul_mx(
                         out=acc[:, 0:256],
@@ -263,10 +279,13 @@ def tile_gnn_kernel(tc, p_nodes, h_nodes, f_nodes, xp, h_att, Wu, Wl, gamma_u, b
             if s == 0:
                 for t in range(2):
                     nc.scalar.activation(
-                        out=y_sb[t][:, cols], in_=y_bank[(t, s)][:], func=ACT.Identity, accum_out=sums[t][:, 0:1]
+                        out=y_sb[t][:, 0:SHIFT_PIX],
+                        in_=y_bank[(t, s)][:, 0:SHIFT_PIX],
+                        func=ACT.Identity,
+                        accum_out=sums[t][:, 0:1],
                     )
                 for t in range(2):
-                    nc.scalar.activation(out=negc[t][:], in_=sums[t][:, 0:1], func=ACT.Identity, scale=-1.0 / 512.0)
+                    nc.scalar.activation(out=negc[t][:], in_=sums[t][:, 0:1], func=ACT.Identity, scale=-1.0 / SHIFT_PIX)
             for t in range(2):
                 nc.scalar.activation(
                     out=o_sb[t][:, cols],
@@ -386,65 +405,68 @@ def tile_gnn_kernel(tc, p_nodes, h_nodes, f_nodes, xp, h_att, Wu, Wl, gamma_u, b
                     w_transpose(t)
                 for t in range(3):
                     w_copy(t)
-            if k == 3:
+            if k == 4:
                 for t in range(3):
                     w_quantise(t)
+                convolve(0, 0)
+                convolve(1, 0)
             if k == 5:
                 upper_squares(0)
-            if k == 6:
-                upper_squares(1)
+                take_out(1, 0)
             if k == 7:
-                upper_squares(2)
+                upper_squares(1)
+            if k == 8:
+                node0_sum(0)
+                node0_sum(1)
             if k == 9:
+                upper_squares(2)
+                node0_out(0)
+                node0_out(1)
+                nc.sync.dma_start(out=out[0].rearrange("b c h w -> (b c) (h w)"), in_=o0[:])
+            if k == 11:
                 upper_means()
                 upper_squares(3)
                 upper_means_out()
                 statistics((0, 1))
                 convolve_tile(0, 0, 0)
                 convolve_tile(0, 0, 1)
-            if k == 10:
+            if k == 12:
                 relu_bank(0, 0)
                 relu_bank(0, 1)
                 convolve_tile(0, 0, 2)
                 convolve_tile(0, 0, 3)
-            if k == 11:
-                take_out(1, 0)
+            if k == 13:
+                take_out(1, 1)
                 relu_bank(0, 2)
                 relu_bank(0, 3)
                 convolve_tile(1, 0, 0)
                 convolve_tile(1, 0, 1)
-            if k == 12:
+            if k == 14:
                 relu_bank(1, 0)
                 relu_bank(1, 1)
-                node0_sum(0)
-                node0_sum(1)
-            if k == 13:
-                take_out(1, 1)
-                node0_out(0)
-                node0_out(1)
-                nc.sync.dma_start(out=out[0].rearrange("b c h w -> (b c) (h w)"), in_=o0[:])
                 convolve_tile(1, 0, 2)
                 convolve_tile(1, 0, 3)
-            if k == 14:
-                relu_bank(1, 2)
-                relu_bank(1, 3)
             if k == 15:
                 take_out(1, 2)
+                relu_bank(1, 2)
+                relu_bank(1, 3)
 
+        spread_at = {0: 2, 3: 3, 4: 4, 6: 5, 8: 6, 10: 7}
+        share_at = {0: 3, 3: 4, 4: 5, 5: 6, 6: 7}
         acc = ps_acc.tile([P, 512], F32, name="acc")
-        spread_att(0, 0)
-        spread_att(0, 1)
+        att_bank[(0, 0)], att_bank[(1, 0)] = first_banks
         if G_PIX > 0:
             for i in range(8):
                 if 2 * i not in V_UNITS:
                     gpsimd_share(i)
-        for i in range(LOOKAHEAD):
+        for i in range(3):
             scalar_share(i)
         for k in range(16):
             a, s, g = halves[k]
-            scalar_share(k + LOOKAHEAD)
-            if g == 0 and k + 4 < 16:
-                spread_att(halves[k + 4][0], halves[k + 4][1])
+            if k in share_at:
+                scalar_share(share_at[k])
+            if k in spread_at:
+                spread_att(blocks[spread_at[k]][0], blocks[spread_at[k]][1])
             if k == 0:
                 for q in range(2):
                     regroup_runs(nc.vector.tensor_copy, k, 256 * q, 256)
@@ -452,9 +474,7 @@ def tile_gnn_kernel(tc, p_nodes, h_nodes, f_nodes, xp, h_att, Wu, Wl, gamma_u, b
             else:
                 multiply(k, 0, 512)
                 quantise(k - 1)
-            if k == 4:
-                convolve(0, 0)
-            if g == 0 and k >= 4:
+            if g == 0 and k >= 6:
                 convolve(halves[k - 2][0], halves[k - 2][1])
             fill(k)
         quantise(15)

@@ -34,8 +34,8 @@ def tile_gnn_kernel(tc, p_nodes, h_nodes, f_nodes, xp, h_att, Wu, Wl, gamma_u, b
 
         xr = [keep.tile([P, 4, 512], BF16, name="xr%d" % i) for i in range(8)]
         xg = [keep.tile([P, 512, 4], BF16, name="xg%d" % i) for i in range(8)]
-        xc = [keep.tile([P, 512], U32, name="xc%d" % k, align_bytes=64) for k in range(16)]
-        xs = [keep.tile([P, 512], U8, name="xs%d" % k, align_bytes=64) for k in range(16)]
+        xc = [keep.tile([P, 1024], U32, name="xc%d" % k, align_bytes=64) for k in range(8)]
+        xs = [keep.tile([P, 1024], U8, name="xs%d" % k, align_bytes=64) for k in range(8)]
         w_sb = [keep.tile([P, 1024], BF16, name="w_sb%d" % t) for t in range(3)]
         wg = keep.tile([P, 2, 3, 512], BF16, name="wg", align_bytes=64)
         wc = keep.tile([P, 768], U32, name="wc", align_bytes=64)
@@ -68,6 +68,11 @@ def tile_gnn_kernel(tc, p_nodes, h_nodes, f_nodes, xp, h_att, Wu, Wl, gamma_u, b
         g0 = keep.tile([P, P], BF16, name="g0")
         g1 = keep.tile([P, P], BF16, name="g1")
         gb = keep.tile([P, 6], F32, name="gb")
+        stats2 = keep.tile([P, 9], F32, name="stats2")
+        mv2 = keep.tile([P, 2], F32, name="mv2")
+        ngm = keep.tile([P, 1], F32, name="ngm")
+        ngam = keep.tile([P, 1], F32, name="ngam")
+        eps1 = keep.tile([P, 1], F32, name="eps1")
         eps4 = keep.tile([P, 1], F32, name="eps4")
         warm = keep.tile([P, 1], F32, name="warm")
 
@@ -75,6 +80,8 @@ def tile_gnn_kernel(tc, p_nodes, h_nodes, f_nodes, xp, h_att, Wu, Wl, gamma_u, b
         nc.vector.memset(a0[64:P, :], 0.0)
         nc.vector.memset(g0[:], 0.0)
         nc.vector.memset(eps4[:], EPS / 4.0)
+        nc.vector.memset(eps1[:], EPS)
+        nc.vector.memset(stats2[:, 0:1], 1536.0)
         nc.vector.memset(ones[:], 1.0)
         nc.sync.dma_start(out=a0[0:32, :], in_=h_att[1:3].rearrange("a b o (hh r) w -> (a b o hh) (r w)", r=4))
         nc.scalar.dma_start(out=g0[0:2, :], in_=gamma_u.rearrange("(r c) -> r c", c=P))
@@ -131,15 +138,14 @@ def tile_gnn_kernel(tc, p_nodes, h_nodes, f_nodes, xp, h_att, Wu, Wl, gamma_u, b
                 )
             return bank[:]
 
-        first_banks = [spread_rows(0, 0), spread_rows(1, 0)]
-        nc.gpsimd.tensor_copy(out=a1[:], in_=a0[:].unsqueeze(2).to_broadcast([P, P, 2]))
         att_t = ps_att.tile([P, 512], F32, name="att_t", tag="att")
+        first_banks = [spread_rows(0, 0)]
+        nc.scalar.copy(out=a1[:], in_=a0[:].unsqueeze(2).to_broadcast([P, P, 2]))
         nc.tensor.transpose(att_t[:, 0:P], a1[:].rearrange("p w j -> p (w j)").bitcast(F32), ident_f[:])
         nc.scalar.copy(out=att_p[:], in_=att_t[:, 0:P])
 
         blocks = [(0, 0), (1, 0), (0, 1), (0, 2), (0, 3), (1, 1), (1, 2), (1, 3)]
-        halves = [(a, 0, g) for g in range(2) for a in range(2)] + [(a, s, g) for a, s in blocks[2:] for g in range(2)]
-        step_of = {half: k for k, half in enumerate(halves)}
+        place = {block: b for b, block in enumerate(blocks)}
         att_bank = {}
         prod = {}
         y_bank = {}
@@ -182,34 +188,29 @@ def tile_gnn_kernel(tc, p_nodes, h_nodes, f_nodes, xp, h_att, Wu, Wl, gamma_u, b
                 )
             att_bank[(a, s)] = bank[:].bitcast(BF16)
 
-        def multiply(k, lo, n):
-            a, s, g = halves[k]
-            if lo == 0:
-                prod[k] = prods.tile([P, 2048], BF16, name="prod", tag="prod", align_bytes=64)
+        def multiply(b, g):
+            a, s = blocks[b]
+            if g == 0:
+                prod[b] = prods.tile([P, 4096], BF16, name="prod", tag="prod", align_bytes=64)
             nc.vector.tensor_tensor(
-                out=prod[k][:, 4 * lo : 4 * (lo + n)].rearrange("p (w u e) -> p w u e", u=2, e=2),
-                in0=xg[2 * s + g][:, lo : lo + n, :].rearrange("p w (u e) -> p w u e", e=2),
-                in1=att_bank[(a, s)][:, 2 * lo : 2 * (lo + n)]
-                .rearrange("p (w e) -> p w e", e=2)
-                .unsqueeze(2)
-                .to_broadcast([P, n, 2, 2]),
+                out=prod[b][:, 2048 * g : 2048 * g + 2048].rearrange("p (w u e) -> p w u e", u=2, e=2),
+                in0=xg[2 * s + g][:].rearrange("p w (u e) -> p w u e", e=2),
+                in1=att_bank[(a, s)].rearrange("p (w e) -> p w e", e=2).unsqueeze(2).to_broadcast([P, 512, 2, 2]),
                 op=ALU.mult,
             )
 
-        def quantise(k):
-            nc.vector.quantize_mx(out=xc[k][:].bitcast(FP8X4), scales=xs[k][:], in_=prod[k][:])
+        def quantise(b):
+            nc.vector.quantize_mx(out=xc[b][:].bitcast(FP8X4), scales=xs[b][:], in_=prod[b][:])
 
         def gains():
-            nc.vector.tensor_copy(
+            nc.scalar.copy(
                 out=g1[:].rearrange("r (c jj) -> r c jj", jj=2), in_=g0[:].rearrange("r (jj c) -> r c jj", jj=2)
             )
+            nc.scalar.activation(out=half_i[:], in_=ident_b[:], func=ACT.Copy, scale=0.5)
             g_t = ps_y.tile([P, 1024], BF16, name="g_t", tag="y")
             nc.tensor.transpose(g_t[:, 0:P], g1[:], ident_b[:])
-            y_bank["g"] = g_t
-
-        def gains_out():
-            nc.vector.tensor_scalar(out=gb[:], in0=y_bank["g"][:, 0:6], scalar1=0.5, scalar2=None, op0=ALU.mult)
-            nc.vector.tensor_scalar(out=half_i[:], in0=ident_f[:], scalar1=0.5, scalar2=None, op0=ALU.mult)
+            nc.scalar.activation(out=gb[:], in_=g_t[:, 0:6], func=ACT.Copy, scale=0.5)
+            nc.scalar.activation(out=ngam[:], in_=g_t[:, 2:3], func=ACT.Copy, scale=-0.5)
 
         def w_transpose(t):
             bank = ps_y.tile([P, 512], F32, name="w_bank", tag="y")
@@ -239,14 +240,14 @@ def tile_gnn_kernel(tc, p_nodes, h_nodes, f_nodes, xp, h_att, Wu, Wl, gamma_u, b
         def convolve_tile(t, a, s):
             bank = ps_y.tile([P, 512], F32, name="y_bank", tag="y")
             for g in range(2):
-                k = step_of[(a, s, g)]
+                b = place[(a, s)]
                 w0 = 384 * g + P * t
                 nc.tensor.matmul_mx(
                     out=bank[:],
                     lhsT=wc[:, w0 : w0 + P].bitcast(FP8X4),
                     lhsT_scale=ws[:, w0 : w0 + P],
-                    rhs=xc[k][:].bitcast(FP8X4),
-                    rhs_scale=xs[k][:],
+                    rhs=xc[b][:, 512 * g : 512 * g + 512].bitcast(FP8X4),
+                    rhs_scale=xs[b][:, 512 * g : 512 * g + 512],
                     start=(g == 0),
                     stop=(g == 1),
                 )
@@ -254,12 +255,13 @@ def tile_gnn_kernel(tc, p_nodes, h_nodes, f_nodes, xp, h_att, Wu, Wl, gamma_u, b
 
         def sum_pixels(s):
             for g in range(2):
-                k = step_of[(0, s, g)]
+                b = place[(0, s)]
                 for m in range(4):
+                    x0 = 512 * g + P * m
                     nc.tensor.matmul_mx(
                         out=acc[:, 0:256],
-                        lhsT=xc[k][:, P * m : P * m + P].bitcast(FP8X4),
-                        lhsT_scale=xs[k][:, P * m : P * m + P],
+                        lhsT=xc[b][:, x0 : x0 + P].bitcast(FP8X4),
+                        lhsT_scale=xs[b][:, x0 : x0 + P],
                         rhs=wc[:, 384 * g : 384 * g + 256].bitcast(FP8X4),
                         rhs_scale=ws[:, 384 * g : 384 * g + 256],
                         start=(s == 0 and g == 0 and m == 0),
@@ -325,11 +327,6 @@ def tile_gnn_kernel(tc, p_nodes, h_nodes, f_nodes, xp, h_att, Wu, Wl, gamma_u, b
                 nc.scalar.activation(
                     out=y_sb[t][:, cols], in_=y_bank[(t, s)][:], func=ACT.Identity, accum_out=sums[t][:, s : s + 1]
                 )
-            if s == 3:
-                for t in o_tiles(a):
-                    nc.scalar.activation(
-                        out=junk_a[t][:], in_=sums[t][:], func=ACT.Identity, scale=-1.0 / NPIX, accum_out=negmean[t][:]
-                    )
             if s == 0:
                 for t in o_tiles(a):
                     nc.scalar.activation(out=negc[t][:], in_=sums[t][:, 0:1], func=ACT.Identity, scale=-1.0 / 512.0)
@@ -341,6 +338,26 @@ def tile_gnn_kernel(tc, p_nodes, h_nodes, f_nodes, xp, h_att, Wu, Wl, gamma_u, b
                     bias=negc[t][:],
                     accum_out=sqs[t][:, s : s + 1],
                 )
+
+        def lower_part_stats():
+            nc.scalar.activation(
+                out=junk_a[2][:, 0:3], in_=sums[2][:, 0:3], func=ACT.Identity, scale=1.0 / 1536.0, accum_out=stats2[:, 1:2]
+            )
+            nc.scalar.activation(
+                out=junk_b[2][:, 0:3], in_=sqs[2][:, 0:3], func=ACT.Identity, accum_out=msq[2][:]
+            )
+            nc.scalar.activation(out=dsq[2][:], in_=stats2[:, 1:2], func=ACT.Square, bias=negc[2][:])
+            nc.scalar.activation(
+                out=stats2[:, 2:3], in_=dsq[2][:], func=ACT.Identity, scale=-1536.0, bias=msq[2][:]
+            )
+
+        def lower_stats():
+            nc.vector.bn_stats(out=stats2[:, 3:9], in_=y_bank[(2, 3)][:])
+            nc.vector.bn_aggr(out=mv2[:], in_=stats2[:])
+            nc.scalar.activation(out=rstd[2][:], in_=mv2[:, 1:2], func=ACT.Abs_reciprocal_sqrt, bias=eps1[:])
+            nc.scalar.activation(out=ngm[:], in_=mv2[:, 0:1], func=ACT.Identity, scale=ngam[:])
+            nc.scalar.activation(out=scl[2][:], in_=gb[:, 2:3], func=ACT.Identity, scale=rstd[2][:])
+            nc.scalar.activation(out=bia[2][:], in_=ngm[:], func=ACT.Identity, scale=rstd[2][:], bias=gb[:, 5:6])
 
         def statistics(tiles):
             for t in tiles:
@@ -380,6 +397,9 @@ def tile_gnn_kernel(tc, p_nodes, h_nodes, f_nodes, xp, h_att, Wu, Wl, gamma_u, b
                 op0=ALU.mult,
                 op1=ALU.add,
             )
+
+        def store(t, lo, n):
+            b, w0 = divmod(lo, 1024)
             for jj in range(2):
                 nc.sync.dma_start(
                     out=out[1 + 2 * t + jj, b].rearrange("c h w -> c (h w)")[:, w0 : w0 + n],
@@ -395,95 +415,108 @@ def tile_gnn_kernel(tc, p_nodes, h_nodes, f_nodes, xp, h_att, Wu, Wl, gamma_u, b
         def node0_out(h):
             nc.scalar.copy(out=o0[:, 512 * h : 512 * h + 512], in_=y_bank[("o0", h)][:])
 
-        def fill(k):
-            if k == 0:
-                gains()
-            if k == 1:
-                gains_out()
-            if k == 2:
-                for t in range(3):
-                    w_transpose(t)
-                for t in range(3):
-                    w_copy(t)
-            if k == 4:
-                for t in range(3):
-                    w_quantise(t)
-                convolve(0, 0)
-                convolve(1, 0)
-            if k == 5:
-                upper_squares(0)
-                take_out(1, 0)
-            if k == 7:
-                upper_squares(1)
-            if k == 8:
-                node0_sum(0)
-                node0_sum(1)
-            if k == 9:
-                upper_squares(2)
-                node0_out(0)
-                node0_out(1)
-                nc.sync.dma_start(out=out[0].rearrange("b c h w -> (b c) (h w)"), in_=o0[:])
-            if k == 11:
-                upper_means()
-                upper_squares(3)
-                upper_means_out()
-                statistics((0, 1))
-                convolve_tile(0, 0, 0)
-                convolve_tile(0, 0, 1)
-            if k == 12:
-                relu_bank(0, 0)
-                relu_bank(0, 1)
-                convolve_tile(0, 0, 2)
-                convolve_tile(0, 0, 3)
-            if k == 13:
-                take_out(1, 1)
-                relu_bank(0, 2)
-                relu_bank(0, 3)
-                convolve_tile(1, 0, 0)
-                convolve_tile(1, 0, 1)
-            if k == 14:
-                relu_bank(1, 0)
-                relu_bank(1, 1)
-                convolve_tile(1, 0, 2)
-                convolve_tile(1, 0, 3)
-            if k == 15:
-                take_out(1, 2)
-                relu_bank(1, 2)
-                relu_bank(1, 3)
-
-        spread_at = {0: 2, 3: 3, 4: 4, 6: 5, 8: 6, 10: 7}
-        share_at = {0: 3, 3: 4, 4: 5, 5: 6, 6: 7}
         acc = ps_acc.tile([P, 512], F32, name="acc")
-        att_bank[(0, 0)], att_bank[(1, 0)] = first_banks
-        if G_PIX > 0:
-            for i in range(8):
-                if 2 * i not in V_UNITS:
-                    gpsimd_share(i)
-        for i in range(3):
+        att_bank[(0, 0)] = first_banks[0]
+        spread_att(1, 0)
+        for i in range(1, 8):
+            gpsimd_share(i)
+        for i in range(1, 4):
             scalar_share(i)
-        for k in range(16):
-            a, s, g = halves[k]
-            if k in share_at:
-                scalar_share(share_at[k])
-            if k in spread_at:
-                spread_att(blocks[spread_at[k]][0], blocks[spread_at[k]][1])
-            if k == 0:
-                for q in range(2):
-                    regroup_runs(nc.vector.tensor_copy, k, 256 * q, 256)
-                multiply(k, 0, 512)
-            else:
-                multiply(k, 0, 512)
-                quantise(k - 1)
-            if g == 0 and k >= 6:
-                convolve(halves[k - 2][0], halves[k - 2][1])
-            fill(k)
-        quantise(15)
+        spread_att(0, 1)
+        for q in range(2):
+            regroup_runs(nc.vector.tensor_copy, 0, 256 * q, 256)
+        multiply(0, 0)
+        multiply(1, 0)
+        multiply(0, 1)
+        for t in range(3):
+            w_transpose(t)
+        for t in range(3):
+            w_copy(t)
+        gains()
+        spread_att(0, 2)
+        multiply(1, 1)
+        quantise(0)
+        scalar_share(4)
+        scalar_share(5)
+        spread_att(0, 3)
+        multiply(2, 0)
+        for t in range(3):
+            w_quantise(t)
+        convolve(0, 0)
+        quantise(1)
+        multiply(2, 1)
+        scalar_share(6)
+        upper_squares(0)
+        scalar_share(7)
+        convolve(1, 0)
+        take_out(1, 0)
+        spread_att(1, 1)
+        multiply(3, 0)
+        quantise(2)
+        multiply(3, 1)
+        convolve(0, 1)
+        upper_squares(1)
+        spread_att(1, 2)
+        multiply(4, 0)
+        quantise(3)
+        multiply(4, 1)
+        convolve(0, 2)
+        upper_squares(2)
+        node0_sum(0)
+        node0_sum(1)
+        node0_out(0)
+        node0_out(1)
+        nc.sync.dma_start(out=out[0].rearrange("b c h w -> (b c) (h w)"), in_=o0[:])
+        spread_att(1, 3)
+        multiply(5, 0)
+        quantise(4)
+        multiply(5, 1)
+        convolve(0, 3)
+        upper_means()
+        upper_squares(3)
+        upper_means_out()
+        statistics((0, 1))
+        convolve_tile(0, 0, 0)
+        convolve_tile(0, 0, 1)
+        relu_bank(0, 0)
+        relu_bank(0, 1)
+        convolve_tile(0, 0, 2)
+        convolve_tile(0, 0, 3)
+        multiply(6, 0)
+        quantise(5)
+        multiply(6, 1)
+        convolve(1, 1)
+        relu_bank(0, 2)
+        relu_bank(0, 3)
+        take_out(1, 1)
+        convolve_tile(1, 0, 0)
+        convolve_tile(1, 0, 1)
+        multiply(7, 0)
+        quantise(6)
+        multiply(7, 1)
+        relu_bank(1, 0)
+        relu_bank(1, 1)
+        convolve(1, 2)
+        convolve_tile(1, 0, 2)
+        convolve_tile(1, 0, 3)
+        take_out(1, 2)
+        lower_part_stats()
+        relu_bank(1, 2)
+        relu_bank(1, 3)
+        for b in range(2):
+            average(0, 1024 * b, 1024)
+            store(0, 1024 * b, 1024)
+        quantise(7)
         convolve(1, 3)
-        take_out(1, 3)
-        statistics((2,))
-        for t in range(2):
-            for b in range(2):
-                average(t, 1024 * b, 1024)
-        for c in range(4):
+        average(1, 0, 512)
+        store(1, 0, 512)
+        lower_stats()
+        for c in range(1, 4):
+            average(1, 512 * c, 512)
+            store(1, 512 * c, 512)
+        for c in range(3):
             relu(2, 512 * c, 512)
+        relu_bank(2, 3)
+        for c in range(4):
             average(2, 512 * c, 512)
+            store(2, 512 * c, 512)

@@ -37,11 +37,11 @@ def tile_gnn_kernel(tc, p_nodes, h_nodes, f_nodes, xp, h_att, Wu, Wl, gamma_u, b
         xc = [keep.tile([P, 1024], U32, name="xc%d" % k, align_bytes=64) for k in range(8)]
         xs = [keep.tile([P, 1024], U8, name="xs%d" % k, align_bytes=64) for k in range(8)]
         w_sb = [keep.tile([P, 1024], BF16, name="w_sb%d" % t) for t in range(3)]
-        wg = keep.tile([P, 2, 3, 512], BF16, name="wg", align_bytes=64)
+        wg = keep.tile([P, 3072], BF16, name="wg", align_bytes=64)
         wc = keep.tile([P, 768], U32, name="wc", align_bytes=64)
         ws = keep.tile([P, 768], U8, name="ws", align_bytes=64)
         acc_sb = keep.tile([P, 256], F32, name="acc_sb")
-        ones = keep.tile([P, 1], F32, name="ones")
+        minus_nth = keep.tile([P, 1], F32, name="minus_nth")
         y_sb = [keep.tile([P, NPIX], F32, name="y_sb%d" % t) for t in range(3)]
         o_sb = [keep.tile([P, NPIX], F32, name="o_sb%d" % t) for t in range(3)]
         pn = [keep.tile([P, 2, 1024], BF16, name="pn%d" % t) for t in range(3)]
@@ -50,7 +50,7 @@ def tile_gnn_kernel(tc, p_nodes, h_nodes, f_nodes, xp, h_att, Wu, Wl, gamma_u, b
         junk_a = [keep.tile([P, 4], F32, name="junk_a%d" % t) for t in range(3)]
         junk_b = [keep.tile([P, 4], F32, name="junk_b%d" % t) for t in range(3)]
         negc = [keep.tile([P, 1], F32, name="negc%d" % t) for t in range(3)]
-        negmean = [keep.tile([P, 1], F32, name="negmean%d" % t) for t in range(3)]
+        posc = [keep.tile([P, 1], F32, name="posc%d" % t) for t in range(2)]
         msq = [keep.tile([P, 1], F32, name="msq%d" % t) for t in range(3)]
         dsq = [keep.tile([P, 1], F32, name="dsq%d" % t) for t in range(3)]
         rstd = [keep.tile([P, 1], F32, name="rstd%d" % t) for t in range(3)]
@@ -70,7 +70,7 @@ def tile_gnn_kernel(tc, p_nodes, h_nodes, f_nodes, xp, h_att, Wu, Wl, gamma_u, b
         gb = keep.tile([P, 6], F32, name="gb")
         stats2 = keep.tile([P, 9], F32, name="stats2")
         mv2 = keep.tile([P, 2], F32, name="mv2")
-        ngm = keep.tile([P, 1], F32, name="ngm")
+        ngm = [keep.tile([P, 1], F32, name="ngm%d" % t) for t in range(3)]
         ngam = keep.tile([P, 1], F32, name="ngam")
         eps1 = keep.tile([P, 1], F32, name="eps1")
         eps4 = keep.tile([P, 1], F32, name="eps4")
@@ -82,7 +82,7 @@ def tile_gnn_kernel(tc, p_nodes, h_nodes, f_nodes, xp, h_att, Wu, Wl, gamma_u, b
         nc.vector.memset(eps4[:], EPS / 4.0)
         nc.vector.memset(eps1[:], EPS)
         nc.vector.memset(stats2[:, 0:1], 1536.0)
-        nc.vector.memset(ones[:], 1.0)
+        nc.vector.memset(minus_nth[:], -1.0 / NPIX)
         nc.sync.dma_start(out=a0[0:32, :], in_=h_att[1:3].rearrange("a b o (hh r) w -> (a b o hh) (r w)", r=4))
         nc.scalar.dma_start(out=g0[0:2, :], in_=gamma_u.rearrange("(r c) -> r c", c=P))
         nc.scalar.dma_start(out=g0[2:3, :], in_=gamma_l.rearrange("(r c) -> r c", c=P))
@@ -225,23 +225,28 @@ def tile_gnn_kernel(tc, p_nodes, h_nodes, f_nodes, xp, h_att, Wu, Wl, gamma_u, b
             y_bank[("w", t)] = bank
 
         def w_copy(t):
+            if t < 2:
+                dst = wg[:, 0:2048].rearrange("p (g t c) -> p g t c", g=2, t=2)[:, :, t, :]
+            else:
+                dst = wg[:, 2048:3072].rearrange("p (g c) -> p g c", g=2)
             nc.scalar.copy(
-                out=wg[:, :, t, :].bitcast(F32).rearrange("p g (o u) -> p g o u", u=2),
+                out=dst.bitcast(F32).rearrange("p g (o u) -> p g o u", u=2),
                 in_=y_bank[("w", t)][:].rearrange("p (g u o) -> p g o u", g=2, u=2),
             )
 
-        def w_quantise(t):
+        def w_quantise(lo, n):
             nc.vector.quantize_mx(
-                out=wc[:, 256 * t : 256 * t + 256].bitcast(FP8X4),
-                scales=ws[:, 256 * t : 256 * t + 256],
-                in_=wg[:].rearrange("p g t c -> p (g t c)")[:, 1024 * t : 1024 * t + 1024],
+                out=wc[:, lo : lo + n].bitcast(FP8X4), scales=ws[:, lo : lo + n], in_=wg[:, 4 * lo : 4 * (lo + n)]
             )
+
+        def w_col(t, g):
+            return 256 * g + P * t if t < 2 else 512 + P * g
 
         def convolve_tile(t, a, s):
             bank = ps_y.tile([P, 512], F32, name="y_bank", tag="y")
             for g in range(2):
                 b = place[(a, s)]
-                w0 = 384 * g + P * t
+                w0 = w_col(t, g)
                 nc.tensor.matmul_mx(
                     out=bank[:],
                     lhsT=wc[:, w0 : w0 + P].bitcast(FP8X4),
@@ -262,8 +267,8 @@ def tile_gnn_kernel(tc, p_nodes, h_nodes, f_nodes, xp, h_att, Wu, Wl, gamma_u, b
                         out=acc[:, 0:256],
                         lhsT=xc[b][:, x0 : x0 + P].bitcast(FP8X4),
                         lhsT_scale=xs[b][:, x0 : x0 + P],
-                        rhs=wc[:, 384 * g : 384 * g + 256].bitcast(FP8X4),
-                        rhs_scale=ws[:, 384 * g : 384 * g + 256],
+                        rhs=wc[:, 256 * g : 256 * g + 256].bitcast(FP8X4),
+                        rhs_scale=ws[:, 256 * g : 256 * g + 256],
                         start=(s == 0 and g == 0 and m == 0),
                         stop=(s == 3 and g == 1 and m == 3),
                     )
@@ -288,6 +293,8 @@ def tile_gnn_kernel(tc, p_nodes, h_nodes, f_nodes, xp, h_att, Wu, Wl, gamma_u, b
                     )
                 for t in range(2):
                     nc.scalar.activation(out=negc[t][:], in_=sums[t][:, 0:1], func=ACT.Identity, scale=-1.0 / SHIFT_PIX)
+                for t in range(2):
+                    nc.scalar.activation(out=posc[t][:], in_=sums[t][:, 0:1], func=ACT.Identity, scale=1.0 / SHIFT_PIX)
             for t in range(2):
                 nc.scalar.activation(
                     out=o_sb[t][:, cols],
@@ -302,15 +309,16 @@ def tile_gnn_kernel(tc, p_nodes, h_nodes, f_nodes, xp, h_att, Wu, Wl, gamma_u, b
             bank = ps_y.tile([P, 512], F32, name="mean_bank", tag="y")
             for t in range(2):
                 nc.tensor.matmul(
-                    out=bank[:, t : t + 1], lhsT=acc_sb[:, P * t : P * t + P], rhs=ones[:], start=True, stop=True
+                    out=bank[:, t : t + 1], lhsT=acc_sb[:, P * t : P * t + P], rhs=minus_nth[:], start=True, stop=True
                 )
             y_bank["mean"] = bank
 
         def upper_means_out():
+            bank = y_bank["mean"]
             for t in range(2):
-                nc.scalar.activation(
-                    out=negmean[t][:], in_=y_bank["mean"][:, t : t + 1], func=ACT.Identity, scale=-1.0 / NPIX
-                )
+                nc.scalar.activation(out=dsq[t][:], in_=bank[:, t : t + 1], func=ACT.Square, bias=posc[t][:])
+            for t in range(2):
+                nc.scalar.activation(out=ngm[t][:], in_=bank[:, t : t + 1], func=ACT.Identity, scale=gb[:, t : t + 1])
 
         def relu_bank(t, s):
             nc.scalar.activation(
@@ -355,13 +363,11 @@ def tile_gnn_kernel(tc, p_nodes, h_nodes, f_nodes, xp, h_att, Wu, Wl, gamma_u, b
             nc.vector.bn_stats(out=stats2[:, 3:9], in_=y_bank[(2, 3)][:])
             nc.vector.bn_aggr(out=mv2[:], in_=stats2[:])
             nc.scalar.activation(out=rstd[2][:], in_=mv2[:, 1:2], func=ACT.Abs_reciprocal_sqrt, bias=eps1[:])
-            nc.scalar.activation(out=ngm[:], in_=mv2[:, 0:1], func=ACT.Identity, scale=ngam[:])
+            nc.scalar.activation(out=ngm[2][:], in_=mv2[:, 0:1], func=ACT.Identity, scale=ngam[:])
             nc.scalar.activation(out=scl[2][:], in_=gb[:, 2:3], func=ACT.Identity, scale=rstd[2][:])
-            nc.scalar.activation(out=bia[2][:], in_=ngm[:], func=ACT.Identity, scale=rstd[2][:], bias=gb[:, 5:6])
+            nc.scalar.activation(out=bia[2][:], in_=ngm[2][:], func=ACT.Identity, scale=rstd[2][:], bias=gb[:, 5:6])
 
         def statistics(tiles):
-            for t in tiles:
-                nc.scalar.activation(out=dsq[t][:], in_=negc[t][:], func=ACT.Square, scale=-1.0, bias=negmean[t][:])
             for t in tiles:
                 nc.scalar.activation(
                     out=junk_b[t][:],
@@ -379,7 +385,7 @@ def tile_gnn_kernel(tc, p_nodes, h_nodes, f_nodes, xp, h_att, Wu, Wl, gamma_u, b
                 nc.scalar.activation(out=scl[t][:], in_=gb[:, t : t + 1], func=ACT.Identity, scale=rstd[t][:])
             for t in tiles:
                 nc.scalar.activation(
-                    out=bia[t][:], in_=negmean[t][:], func=ACT.Identity, scale=scl[t][:], bias=gb[:, 3 + t : 4 + t]
+                    out=bia[t][:], in_=ngm[t][:], func=ACT.Identity, scale=rstd[t][:], bias=gb[:, 3 + t : 4 + t]
                 )
 
         def relu(t, lo, n):
@@ -440,22 +446,22 @@ def tile_gnn_kernel(tc, p_nodes, h_nodes, f_nodes, xp, h_att, Wu, Wl, gamma_u, b
         scalar_share(5)
         spread_att(0, 3)
         multiply(2, 0)
-        for t in range(3):
-            w_quantise(t)
-        convolve(0, 0)
         quantise(1)
         multiply(2, 1)
+        w_quantise(0, 512)
+        convolve(0, 0)
         scalar_share(6)
         upper_squares(0)
         scalar_share(7)
-        convolve(1, 0)
-        take_out(1, 0)
         spread_att(1, 1)
         multiply(3, 0)
         quantise(2)
         multiply(3, 1)
+        w_quantise(512, 256)
         convolve(0, 1)
         upper_squares(1)
+        convolve(1, 0)
+        take_out(1, 0)
         spread_att(1, 2)
         multiply(4, 0)
         quantise(3)

@@ -18,7 +18,7 @@ P = 128
 EPS = 1e-5
 NPIX = 2048
 V_UNITS = (0, 1)
-G_PIX = 192
+G_SHARE = (0, 224, 192, 192, 192, 192, 192, 192)
 SHIFT_PIX = 64
 
 
@@ -68,7 +68,7 @@ def tile_gnn_kernel(tc, p_nodes, h_nodes, f_nodes, xp, h_att, Wu, Wl, gamma_u, b
         g0 = keep.tile([P, P], BF16, name="g0")
         g1 = keep.tile([P, P], BF16, name="g1")
         gb = keep.tile([P, 6], F32, name="gb")
-        stats2 = keep.tile([P, 9], F32, name="stats2")
+        stats2 = keep.tile([P, 15], F32, name="stats2")
         mv2 = keep.tile([P, 2], F32, name="mv2")
         ngm = [keep.tile([P, 1], F32, name="ngm%d" % t) for t in range(3)]
         ngam = keep.tile([P, 1], F32, name="ngam")
@@ -83,22 +83,17 @@ def tile_gnn_kernel(tc, p_nodes, h_nodes, f_nodes, xp, h_att, Wu, Wl, gamma_u, b
         nc.vector.memset(eps1[:], EPS)
         nc.vector.memset(stats2[:, 0:1], 1536.0)
         nc.vector.memset(minus_nth[:], -1.0 / NPIX)
-        nc.sync.dma_start(out=a0[0:32, :], in_=h_att[1:3].rearrange("a b o (hh r) w -> (a b o hh) (r w)", r=4))
         nc.scalar.dma_start(out=g0[0:2, :], in_=gamma_u.rearrange("(r c) -> r c", c=P))
         nc.scalar.dma_start(out=g0[2:3, :], in_=gamma_l.rearrange("(r c) -> r c", c=P))
         nc.scalar.dma_start(out=g0[3:5, :], in_=beta_u.rearrange("(r c) -> r c", c=P))
         nc.scalar.dma_start(out=g0[5:6, :], in_=beta_l.rearrange("(r c) -> r c", c=P))
         nc.scalar.activation(out=warm[:], in_=eps4[:], func=ACT.Abs_reciprocal_sqrt)
 
-        def load_x(i, parts):
+        def load_x(i, lo, n):
             s, g = divmod(i, 2)
             b, h = divmod(s, 2)
             rows = xp[b, 512 * g : 512 * g + 512].rearrange("(p j) h w -> p j (h w)", j=4)
-            n = 512 // parts
-            for c in range(parts):
-                nc.sync.dma_start(
-                    out=xr[i][:, :, n * c : n * c + n], in_=rows[:, :, 512 * h + n * c : 512 * h + n * c + n]
-                )
+            nc.sync.dma_start(out=xr[i][:, :, lo : lo + n], in_=rows[:, :, 512 * h + lo : 512 * h + lo + n])
 
         def load_w(t):
             for jj in range(2):
@@ -109,13 +104,15 @@ def tile_gnn_kernel(tc, p_nodes, h_nodes, f_nodes, xp, h_att, Wu, Wl, gamma_u, b
             for jj in range(2):
                 nc.sync.dma_start(out=pn[t][jj:P:2, :, :], in_=p_nodes[1 + 2 * t + jj].rearrange("b c h w -> c b (h w)"))
 
-        load_x(0, 2)
+        nc.sync.dma_start(out=a0[0:32, :], in_=h_att[1:3].rearrange("a b o (hh r) w -> (a b o hh) (r w)", r=4))
+        load_x(0, 0, 256)
+        load_x(0, 256, 256)
         for i in range(1, 4):
-            load_x(i, 1)
+            load_x(i, 0, 512)
         for t in range(3):
             load_w(t)
         for i in range(4, 8):
-            load_x(i, 1)
+            load_x(i, 0, 512)
         load_p(0)
         load_p(1)
         nc.sync.dma_start(out=h0[:], in_=h_nodes[0].rearrange("b c h w -> (b c) (h w)"))
@@ -138,11 +135,16 @@ def tile_gnn_kernel(tc, p_nodes, h_nodes, f_nodes, xp, h_att, Wu, Wl, gamma_u, b
                 )
             return bank[:]
 
+        def regroup_runs(engine_copy, i, lo, n):
+            dst = xg[i][:, lo : lo + n, :].rearrange("p (c i) t -> p c t i", i=4)
+            src = xr[i][:, :, lo : lo + n].rearrange("p t (c i) -> p c t i", i=4)
+            engine_copy(out=dst, in_=src)
+
         att_t = ps_att.tile([P, 512], F32, name="att_t", tag="att")
-        first_banks = [spread_rows(0, 0)]
+        first_banks = [spread_rows(0, 0), spread_rows(1, 0)]
         nc.scalar.copy(out=a1[:], in_=a0[:].unsqueeze(2).to_broadcast([P, P, 2]))
+        regroup_runs(nc.scalar.copy, 0, 256, 160)
         nc.tensor.transpose(att_t[:, 0:P], a1[:].rearrange("p w j -> p (w j)").bitcast(F32), ident_f[:])
-        nc.scalar.copy(out=att_p[:], in_=att_t[:, 0:P])
 
         blocks = [(0, 0), (1, 0), (0, 1), (0, 2), (0, 3), (1, 1), (1, 2), (1, 3)]
         place = {block: b for b, block in enumerate(blocks)}
@@ -153,31 +155,15 @@ def tile_gnn_kernel(tc, p_nodes, h_nodes, f_nodes, xp, h_att, Wu, Wl, gamma_u, b
         def o_tiles(a):
             return (0, 1) if a == 0 else (2,)
 
-        def regroup_runs(engine_copy, i, lo, n):
-            dst = xg[i][:, lo : lo + n, :].rearrange("p (c i) t -> p c t i", i=4)
-            src = xr[i][:, :, lo : lo + n].rearrange("p t (c i) -> p c t i", i=4)
-            engine_copy(out=dst, in_=src)
-
-        def gpsimd_share(i):
+        def gpsimd_share(i, lo, n):
             nc.gpsimd.tensor_scalar(
-                out=xg[i][:, 0:G_PIX, :],
-                in0=xr[i][:, :, 0:G_PIX].rearrange("p t w -> p w t"),
+                out=xg[i][:, lo : lo + n, :],
+                in0=xr[i][:, :, lo : lo + n].rearrange("p t w -> p w t"),
                 scalar1=1.0,
                 scalar2=0.0,
                 op0=ALU.mult,
                 op1=ALU.add,
             )
-
-        def scalar_share(i):
-            if i >= 8:
-                return
-            if G_PIX > 0:
-                if 2 * i not in V_UNITS:
-                    regroup_runs(nc.scalar.copy, i, G_PIX, 512 - G_PIX)
-            else:
-                for q in range(2):
-                    if 2 * i + q not in V_UNITS:
-                        regroup_runs(nc.scalar.copy, i, 256 * q, 256)
 
         def spread_att(a, s):
             bank = ps_att.tile([P, 512], F32, name="att_bank", tag="att")
@@ -188,14 +174,18 @@ def tile_gnn_kernel(tc, p_nodes, h_nodes, f_nodes, xp, h_att, Wu, Wl, gamma_u, b
                 )
             att_bank[(a, s)] = bank[:].bitcast(BF16)
 
-        def multiply(b, g):
+        def multiply(b, g, lo=0, n=512):
             a, s = blocks[b]
-            if g == 0:
+            if g == 0 and lo == 0:
                 prod[b] = prods.tile([P, 4096], BF16, name="prod", tag="prod", align_bytes=64)
+            c0 = 2048 * g + 4 * lo
             nc.vector.tensor_tensor(
-                out=prod[b][:, 2048 * g : 2048 * g + 2048].rearrange("p (w u e) -> p w u e", u=2, e=2),
-                in0=xg[2 * s + g][:].rearrange("p w (u e) -> p w u e", e=2),
-                in1=att_bank[(a, s)].rearrange("p (w e) -> p w e", e=2).unsqueeze(2).to_broadcast([P, 512, 2, 2]),
+                out=prod[b][:, c0 : c0 + 4 * n].rearrange("p (w u e) -> p w u e", u=2, e=2),
+                in0=xg[2 * s + g][:, lo : lo + n, :].rearrange("p w (u e) -> p w u e", e=2),
+                in1=att_bank[(a, s)][:, 2 * lo : 2 * (lo + n)]
+                .rearrange("p (w e) -> p w e", e=2)
+                .unsqueeze(2)
+                .to_broadcast([P, n, 2, 2]),
                 op=ALU.mult,
             )
 
@@ -273,6 +263,24 @@ def tile_gnn_kernel(tc, p_nodes, h_nodes, f_nodes, xp, h_att, Wu, Wl, gamma_u, b
                         stop=(s == 3 and g == 1 and m == 3),
                     )
 
+        def convolve_last():
+            for h in range(2):
+                pool, tag = (ps_y, "y") if h == 0 else (ps_att, "att")
+                bank = pool.tile([P, 512], F32, name="last_bank", tag=tag)
+                for g in range(2):
+                    x0 = 512 * g + 256 * h
+                    w0 = w_col(2, g)
+                    nc.tensor.matmul_mx(
+                        out=bank[:, 0:256],
+                        lhsT=wc[:, w0 : w0 + P].bitcast(FP8X4),
+                        lhsT_scale=ws[:, w0 : w0 + P],
+                        rhs=xc[7][:, x0 : x0 + 256].bitcast(FP8X4),
+                        rhs_scale=xs[7][:, x0 : x0 + 256],
+                        start=(g == 0),
+                        stop=(g == 1),
+                    )
+                y_bank[("last", h)] = bank
+
         def convolve(a, s):
             if a == 0 and s == 3:
                 sum_pixels(s)
@@ -329,6 +337,16 @@ def tile_gnn_kernel(tc, p_nodes, h_nodes, f_nodes, xp, h_att, Wu, Wl, gamma_u, b
                 bias=bia[t][:],
             )
 
+        def relu_last(h):
+            lo = 1536 + 256 * h
+            nc.scalar.activation(
+                out=y_sb[2][:, lo : lo + 256],
+                in_=y_bank[("last", h)][:, 0:256],
+                func=ACT.Relu,
+                scale=scl[2][:],
+                bias=bia[2][:],
+            )
+
         def take_out(a, s):
             cols = slice(512 * s, 512 * s + 512)
             for t in o_tiles(a):
@@ -360,7 +378,10 @@ def tile_gnn_kernel(tc, p_nodes, h_nodes, f_nodes, xp, h_att, Wu, Wl, gamma_u, b
             )
 
         def lower_stats():
-            nc.vector.bn_stats(out=stats2[:, 3:9], in_=y_bank[(2, 3)][:])
+            for h in range(2):
+                nc.vector.bn_stats(out=stats2[:, 3 + 6 * h : 9 + 6 * h], in_=y_bank[("last", h)][:, 0:256])
+            average(1, 384, 256)
+            store(1, 384, 256)
             nc.vector.bn_aggr(out=mv2[:], in_=stats2[:])
             nc.scalar.activation(out=rstd[2][:], in_=mv2[:, 1:2], func=ACT.Abs_reciprocal_sqrt, bias=eps1[:])
             nc.scalar.activation(out=ngm[2][:], in_=mv2[:, 0:1], func=ACT.Identity, scale=ngam[:])
@@ -404,6 +425,16 @@ def tile_gnn_kernel(tc, p_nodes, h_nodes, f_nodes, xp, h_att, Wu, Wl, gamma_u, b
                 op1=ALU.add,
             )
 
+        def pe_average(t, lo, n):
+            b, w0 = divmod(lo, 1024)
+            bank = ps_att.tile([P, 512], F32, name="add_bank", tag="att")
+            nc.tensor.matmul(out=bank[:, 0:n], lhsT=half_i[:], rhs=pn[t][:, b, w0 : w0 + n], start=True, stop=False)
+            nc.tensor.matmul(out=bank[:, 0:n], lhsT=ident_f[:], rhs=y_sb[t][:, lo : lo + n], start=False, stop=True)
+            y_bank[("add", t, lo)] = bank
+
+        def pe_average_out(t, lo, n):
+            nc.scalar.copy(out=o_sb[t][:, lo : lo + n], in_=y_bank[("add", t, lo)][:, 0:n])
+
         def store(t, lo, n):
             b, w0 = divmod(lo, 1024)
             for jj in range(2):
@@ -422,16 +453,20 @@ def tile_gnn_kernel(tc, p_nodes, h_nodes, f_nodes, xp, h_att, Wu, Wl, gamma_u, b
             nc.scalar.copy(out=o0[:, 512 * h : 512 * h + 512], in_=y_bank[("o0", h)][:])
 
         acc = ps_acc.tile([P, 512], F32, name="acc")
-        att_bank[(0, 0)] = first_banks[0]
-        spread_att(1, 0)
+        att_bank[(0, 0)], att_bank[(1, 0)] = first_banks
+        gpsimd_share(0, 416, 96)
         for i in range(1, 8):
-            gpsimd_share(i)
-        for i in range(1, 4):
-            scalar_share(i)
+            gpsimd_share(i, 0, G_SHARE[i])
+        regroup_runs(nc.scalar.copy, 1, G_SHARE[1], 512 - G_SHARE[1])
+        nc.scalar.copy(out=att_p[:], in_=att_t[:, 0:P])
+        for i in range(2, 4):
+            regroup_runs(nc.scalar.copy, i, G_SHARE[i], 512 - G_SHARE[i])
         spread_att(0, 1)
-        for q in range(2):
-            regroup_runs(nc.vector.tensor_copy, 0, 256 * q, 256)
-        multiply(0, 0)
+        for c in range(2):
+            regroup_runs(nc.vector.tensor_copy, 0, 128 * c, 128)
+        for c in range(2):
+            multiply(0, 0, 128 * c, 128)
+        multiply(0, 0, 256, 256)
         multiply(1, 0)
         multiply(0, 1)
         for t in range(3):
@@ -442,17 +477,17 @@ def tile_gnn_kernel(tc, p_nodes, h_nodes, f_nodes, xp, h_att, Wu, Wl, gamma_u, b
         spread_att(0, 2)
         multiply(1, 1)
         quantise(0)
-        scalar_share(4)
-        scalar_share(5)
+        regroup_runs(nc.scalar.copy, 4, G_SHARE[4], 512 - G_SHARE[4])
+        regroup_runs(nc.scalar.copy, 5, G_SHARE[5], 512 - G_SHARE[5])
         spread_att(0, 3)
         multiply(2, 0)
-        quantise(1)
-        multiply(2, 1)
         w_quantise(0, 512)
         convolve(0, 0)
-        scalar_share(6)
+        quantise(1)
+        multiply(2, 1)
+        regroup_runs(nc.scalar.copy, 6, G_SHARE[6], 512 - G_SHARE[6])
         upper_squares(0)
-        scalar_share(7)
+        regroup_runs(nc.scalar.copy, 7, G_SHARE[7], 512 - G_SHARE[7])
         spread_att(1, 1)
         multiply(3, 0)
         quantise(2)
@@ -506,23 +541,31 @@ def tile_gnn_kernel(tc, p_nodes, h_nodes, f_nodes, xp, h_att, Wu, Wl, gamma_u, b
         convolve_tile(1, 0, 2)
         convolve_tile(1, 0, 3)
         take_out(1, 2)
+        pe_average(0, 1664, 384)
         lower_part_stats()
         relu_bank(1, 2)
+        pe_average_out(0, 1664, 384)
         relu_bank(1, 3)
-        for b in range(2):
-            average(0, 1024 * b, 1024)
-            store(0, 1024 * b, 1024)
+        average(0, 0, 1024)
+        store(0, 0, 1024)
+        average(0, 1024, 640)
+        store(0, 1024, 640)
         quantise(7)
-        convolve(1, 3)
-        average(1, 0, 512)
-        store(1, 0, 512)
+        convolve_last()
+        average(1, 0, 384)
+        store(1, 0, 384)
+        store(0, 1664, 384)
         lower_stats()
-        for c in range(1, 4):
-            average(1, 512 * c, 512)
-            store(1, 512 * c, 512)
+        average(1, 640, 384)
+        store(1, 640, 384)
+        average(1, 1024, 512)
+        store(1, 1024, 512)
+        average(1, 1536, 512)
+        store(1, 1536, 512)
         for c in range(3):
             relu(2, 512 * c, 512)
-        relu_bank(2, 3)
-        for c in range(4):
-            average(2, 512 * c, 512)
-            store(2, 512 * c, 512)
+        for h in range(2):
+            relu_last(h)
+        for lo, n in ((0, 512), (512, 512), (1024, 512), (1536, 256), (1792, 256)):
+            average(2, lo, n)
+            store(2, lo, n)

from contextlib import ExitStack

import concourse.mybir as mybir
from concourse.masks import make_identity

FLOPS = 2 * 384 * 1024 * 2048
BYTES = 10757632

BF16 = mybir.dt.bfloat16
F32 = mybir.dt.float32
U32 = mybir.dt.uint32
U8 = mybir.dt.uint8
FP8X4 = mybir.dt.float8_e4m3fn_x4
ACT = mybir.ActivationFunctionType
ALU = mybir.AluOpType

P = 128
EPS = 1e-5
NPIX = 2048
V_UNITS = (0, 1)
G_SHARE = (0, 224, 192, 192, 192, 192, 192, 192)
SHIFT_PIX = 64


def tile_gnn_kernel(tc, p_nodes, h_nodes, f_nodes, xp, h_att, Wu, Wl, gamma_u, beta_u, gamma_l, beta_l, out):
    nc = tc.nc
    with ExitStack() as ctx:
        keep = ctx.enter_context(tc.tile_pool(name="keep", bufs=1))
        prods = ctx.enter_context(tc.tile_pool(name="prods", bufs=3))
        ps_att = ctx.enter_context(tc.psum_pool(name="ps_att", bufs=3))
        ps_y = ctx.enter_context(tc.psum_pool(name="ps_y", bufs=4))
        ps_acc = ctx.enter_context(tc.psum_pool(name="ps_acc", bufs=1))
        ctx.enter_context(tc.manual_schedule())

        xr = [keep.tile([P, 4, 512], BF16, name="xr%d" % i) for i in range(8)]
        xg = [keep.tile([P, 512, 4], BF16, name="xg%d" % i) for i in range(8)]
        xc = [keep.tile([P, 1024], U32, name="xc%d" % k, align_bytes=64) for k in range(8)]
        xs = [keep.tile([P, 1024], U8, name="xs%d" % k, align_bytes=64) for k in range(8)]
        w_sb = [keep.tile([P, 1024], BF16, name="w_sb%d" % t) for t in range(3)]
        wg = keep.tile([P, 3072], BF16, name="wg", align_bytes=64)
        wc = keep.tile([P, 768], U32, name="wc", align_bytes=64)
        ws = keep.tile([P, 768], U8, name="ws", align_bytes=64)
        acc_sb = keep.tile([P, 256], F32, name="acc_sb")
        minus_nth = keep.tile([P, 1], F32, name="minus_nth")
        y_sb = [keep.tile([P, NPIX], F32, name="y_sb%d" % t) for t in range(3)]
        o_sb = [keep.tile([P, NPIX], F32, name="o_sb%d" % t) for t in range(3)]
        pn = [keep.tile([P, 2, 1024], BF16, name="pn%d" % t) for t in range(3)]
        sums = [keep.tile([P, 4], F32, name="sums%d" % t) for t in range(3)]
        sqs = [keep.tile([P, 4], F32, name="sqs%d" % t) for t in range(3)]
        junk_a = [keep.tile([P, 4], F32, name="junk_a%d" % t) for t in range(3)]
        junk_b = [keep.tile([P, 4], F32, name="junk_b%d" % t) for t in range(3)]
        negc = [keep.tile([P, 1], F32, name="negc%d" % t) for t in range(3)]
        posc = [keep.tile([P, 1], F32, name="posc%d" % t) for t in range(2)]
        msq = [keep.tile([P, 1], F32, name="msq%d" % t) for t in range(3)]
        dsq = [keep.tile([P, 1], F32, name="dsq%d" % t) for t in range(3)]
        rstd = [keep.tile([P, 1], F32, name="rstd%d" % t) for t in range(3)]
        scl = [keep.tile([P, 1], F32, name="scl%d" % t) for t in range(3)]
        bia = [keep.tile([P, 1], F32, name="bia%d" % t) for t in range(3)]
        h0 = keep.tile([P, 1024], BF16, name="h0")
        p0 = keep.tile([P, 1024], BF16, name="p0")
        o0 = keep.tile([P, 1024], F32, name="o0")
        ident_f = keep.tile([P, P], F32, name="ident_f")
        ident_b = keep.tile([P, P], BF16, name="ident_b")
        half_i = keep.tile([P, P], BF16, name="half_i")
        a0 = keep.tile([P, P], BF16, name="a0")
        a1 = keep.tile([P, P, 2], BF16, name="a1")
        att_p = keep.tile([P, P], F32, name="att_p")
        g0 = keep.tile([P, P], BF16, name="g0")
        g1 = keep.tile([P, P], BF16, name="g1")
        gb = keep.tile([P, 6], F32, name="gb")
        stats2 = keep.tile([P, 15], F32, name="stats2")
        mv2 = keep.tile([P, 2], F32, name="mv2")
        ngm = [keep.tile([P, 1], F32, name="ngm%d" % t) for t in range(3)]
        ngam = keep.tile([P, 1], F32, name="ngam")
        eps1 = keep.tile([P, 1], F32, name="eps1")
        eps4 = keep.tile([P, 1], F32, name="eps4")
        warm = keep.tile([P, 1], F32, name="warm")

        nc.vector.memset(a0[32:64, :], 0.0)
        nc.vector.memset(a0[64:P, :], 0.0)
        nc.vector.memset(g0[:], 0.0)
        nc.vector.memset(eps4[:], EPS / 4.0)
        nc.vector.memset(eps1[:], EPS)
        nc.vector.memset(stats2[:, 0:1], 1536.0)
        nc.vector.memset(minus_nth[:], -1.0 / NPIX)
        nc.scalar.dma_start(out=g0[0:2, :], in_=gamma_u.rearrange("(r c) -> r c", c=P))
        nc.scalar.dma_start(out=g0[2:3, :], in_=gamma_l.rearrange("(r c) -> r c", c=P))
        nc.scalar.dma_start(out=g0[3:5, :], in_=beta_u.rearrange("(r c) -> r c", c=P))
        nc.scalar.dma_start(out=g0[5:6, :], in_=beta_l.rearrange("(r c) -> r c", c=P))
        nc.scalar.activation(out=warm[:], in_=eps4[:], func=ACT.Abs_reciprocal_sqrt)

        def load_x(i, lo, n):
            s, g = divmod(i, 2)
            b, h = divmod(s, 2)
            rows = xp[b, 512 * g : 512 * g + 512].rearrange("(p j) h w -> p j (h w)", j=4)
            nc.sync.dma_start(out=xr[i][:, :, lo : lo + n], in_=rows[:, :, 512 * h + lo : 512 * h + lo + n])

        def load_w(t):
            for jj in range(2):
                rows = Wu[P * t + 64 * jj : P * t + 64 * jj + 64, :] if t < 2 else Wl[64 * jj : 64 * jj + 64, :]
                nc.sync.dma_start(out=w_sb[t][jj:P:2, :], in_=rows)

        def load_p(t):
            for jj in range(2):
                nc.sync.dma_start(out=pn[t][jj:P:2, :, :], in_=p_nodes[1 + 2 * t + jj].rearrange("b c h w -> c b (h w)"))

        nc.sync.dma_start(out=a0[0:32, :], in_=h_att[1:3].rearrange("a b o (hh r) w -> (a b o hh) (r w)", r=4))
        load_x(0, 0, 256)
        load_x(0, 256, 256)
        for i in range(1, 4):
            load_x(i, 0, 512)
        for t in range(3):
            load_w(t)
        for i in range(4, 8):
            load_x(i, 0, 512)
        load_p(0)
        load_p(1)
        nc.sync.dma_start(out=h0[:], in_=h_nodes[0].rearrange("b c h w -> (b c) (h w)"))
        nc.sync.dma_start(out=p0[:], in_=p_nodes[0].rearrange("b c h w -> (b c) (h w)"))
        load_p(2)

        make_identity(nc, ident_b[:])
        make_identity(nc, ident_f[:])

        def spread_rows(a, s):
            bank = ps_att.tile([P, 1024], BF16, name="row_bank", tag="att")
            for r in range(4):
                row = 16 * a + 4 * s + r
                nc.tensor.matmul(
                    out=bank[:, 256 * r : 256 * r + 256],
                    lhsT=ident_b[:, row : row + 1].to_broadcast([P, P]),
                    rhs=a0[:].unsqueeze(2).to_broadcast([P, P, 2]),
                    start=True,
                    stop=True,
                )
            return bank[:]

        def regroup_runs(engine_copy, i, lo, n):
            dst = xg[i][:, lo : lo + n, :].rearrange("p (c i) t -> p c t i", i=4)
            src = xr[i][:, :, lo : lo + n].rearrange("p t (c i) -> p c t i", i=4)
            engine_copy(out=dst, in_=src)

        att_t = ps_att.tile([P, 512], F32, name="att_t", tag="att")
        first_banks = [spread_rows(0, 0), spread_rows(1, 0)]
        nc.scalar.copy(out=a1[:], in_=a0[:].unsqueeze(2).to_broadcast([P, P, 2]))
        regroup_runs(nc.scalar.copy, 0, 256, 160)
        nc.tensor.transpose(att_t[:, 0:P], a1[:].rearrange("p w j -> p (w j)").bitcast(F32), ident_f[:])

        blocks = [(0, 0), (1, 0), (0, 1), (0, 2), (0, 3), (1, 1), (1, 2), (1, 3)]
        place = {block: b for b, block in enumerate(blocks)}
        att_bank = {}
        prod = {}
        y_bank = {}

        def o_tiles(a):
            return (0, 1) if a == 0 else (2,)

        def gpsimd_share(i, lo, n):
            nc.gpsimd.tensor_scalar(
                out=xg[i][:, lo : lo + n, :],
                in0=xr[i][:, :, lo : lo + n].rearrange("p t w -> p w t"),
                scalar1=1.0,
                scalar2=0.0,
                op0=ALU.mult,
                op1=ALU.add,
            )

        def spread_att(a, s):
            bank = ps_att.tile([P, 512], F32, name="att_bank", tag="att")
            for r in range(4):
                row = 16 * a + 4 * s + r
                nc.tensor.transpose(
                    bank[:, P * r : P * r + P], att_p[:, row : row + 1].to_broadcast([P, P]), ident_f[:]
                )
            att_bank[(a, s)] = bank[:].bitcast(BF16)

        def multiply(b, g, lo=0, n=512):
            a, s = blocks[b]
            if g == 0 and lo == 0:
                prod[b] = prods.tile([P, 4096], BF16, name="prod", tag="prod", align_bytes=64)
            c0 = 2048 * g + 4 * lo
            nc.vector.tensor_tensor(
                out=prod[b][:, c0 : c0 + 4 * n].rearrange("p (w u e) -> p w u e", u=2, e=2),
                in0=xg[2 * s + g][:, lo : lo + n, :].rearrange("p w (u e) -> p w u e", e=2),
                in1=att_bank[(a, s)][:, 2 * lo : 2 * (lo + n)]
                .rearrange("p (w e) -> p w e", e=2)
                .unsqueeze(2)
                .to_broadcast([P, n, 2, 2]),
                op=ALU.mult,
            )

        def quantise(b):
            nc.vector.quantize_mx(out=xc[b][:].bitcast(FP8X4), scales=xs[b][:], in_=prod[b][:])

        def gains():
            nc.scalar.copy(
                out=g1[:].rearrange("r (c jj) -> r c jj", jj=2), in_=g0[:].rearrange("r (jj c) -> r c jj", jj=2)
            )
            nc.scalar.activation(out=half_i[:], in_=ident_b[:], func=ACT.Copy, scale=0.5)
            g_t = ps_y.tile([P, 1024], BF16, name="g_t", tag="y")
            nc.tensor.transpose(g_t[:, 0:P], g1[:], ident_b[:])
            nc.scalar.activation(out=gb[:], in_=g_t[:, 0:6], func=ACT.Copy, scale=0.5)
            nc.scalar.activation(out=ngam[:], in_=g_t[:, 2:3], func=ACT.Copy, scale=-0.5)

        def w_transpose(t):
            bank = ps_y.tile([P, 512], F32, name="w_bank", tag="y")
            words = w_sb[t][:].bitcast(F32)
            for g in range(2):
                for u in range(2):
                    nc.tensor.transpose(
                        bank[:, P * (2 * g + u) : P * (2 * g + u) + P],
                        words[:, 256 * g + u : 256 * g + 256 : 2],
                        ident_f[:],
                    )
            y_bank[("w", t)] = bank

        def w_copy(t):
            if t < 2:
                dst = wg[:, 0:2048].rearrange("p (g t c) -> p g t c", g=2, t=2)[:, :, t, :]
            else:
                dst = wg[:, 2048:3072].rearrange("p (g c) -> p g c", g=2)
            nc.scalar.copy(
                out=dst.bitcast(F32).rearrange("p g (o u) -> p g o u", u=2),
                in_=y_bank[("w", t)][:].rearrange("p (g u o) -> p g o u", g=2, u=2),
            )

        def w_quantise(lo, n):
            nc.vector.quantize_mx(
                out=wc[:, lo : lo + n].bitcast(FP8X4), scales=ws[:, lo : lo + n], in_=wg[:, 4 * lo : 4 * (lo + n)]
            )

        def w_col(t, g):
            return 256 * g + P * t if t < 2 else 512 + P * g

        def convolve_tile(t, a, s):
            bank = ps_y.tile([P, 512], F32, name="y_bank", tag="y")
            for g in range(2):
                b = place[(a, s)]
                w0 = w_col(t, g)
                nc.tensor.matmul_mx(
                    out=bank[:],
                    lhsT=wc[:, w0 : w0 + P].bitcast(FP8X4),
                    lhsT_scale=ws[:, w0 : w0 + P],
                    rhs=xc[b][:, 512 * g : 512 * g + 512].bitcast(FP8X4),
                    rhs_scale=xs[b][:, 512 * g : 512 * g + 512],
                    start=(g == 0),
                    stop=(g == 1),
                )
            y_bank[(t, s)] = bank

        def sum_pixels(s):
            for g in range(2):
                b = place[(0, s)]
                for m in range(4):
                    x0 = 512 * g + P * m
                    nc.tensor.matmul_mx(
                        out=acc[:, 0:256],
                        lhsT=xc[b][:, x0 : x0 + P].bitcast(FP8X4),
                        lhsT_scale=xs[b][:, x0 : x0 + P],
                        rhs=wc[:, 256 * g : 256 * g + 256].bitcast(FP8X4),
                        rhs_scale=ws[:, 256 * g : 256 * g + 256],
                        start=(s == 0 and g == 0 and m == 0),
                        stop=(s == 3 and g == 1 and m == 3),
                    )

        def convolve_last():
            for h in range(2):
                pool, tag = (ps_y, "y") if h == 0 else (ps_att, "att")
                bank = pool.tile([P, 512], F32, name="last_bank", tag=tag)
                for g in range(2):
                    x0 = 512 * g + 256 * h
                    w0 = w_col(2, g)
                    nc.tensor.matmul_mx(
                        out=bank[:, 0:256],
                        lhsT=wc[:, w0 : w0 + P].bitcast(FP8X4),
                        lhsT_scale=ws[:, w0 : w0 + P],
                        rhs=xc[7][:, x0 : x0 + 256].bitcast(FP8X4),
                        rhs_scale=xs[7][:, x0 : x0 + 256],
                        start=(g == 0),
                        stop=(g == 1),
                    )
                y_bank[("last", h)] = bank

        def convolve(a, s):
            if a == 0 and s == 3:
                sum_pixels(s)
            for t in o_tiles(a):
                convolve_tile(t, a, s)
            if a == 0 and s < 3:
                sum_pixels(s)

        def upper_squares(s):
            cols = slice(512 * s, 512 * s + 512)
            if s == 0:
                for t in range(2):
                    nc.scalar.activation(
                        out=y_sb[t][:, 0:SHIFT_PIX],
                        in_=y_bank[(t, s)][:, 0:SHIFT_PIX],
                        func=ACT.Identity,
                        accum_out=sums[t][:, 0:1],
                    )
                for t in range(2):
                    nc.scalar.activation(out=negc[t][:], in_=sums[t][:, 0:1], func=ACT.Identity, scale=-1.0 / SHIFT_PIX)
                for t in range(2):
                    nc.scalar.activation(out=posc[t][:], in_=sums[t][:, 0:1], func=ACT.Identity, scale=1.0 / SHIFT_PIX)
            for t in range(2):
                nc.scalar.activation(
                    out=o_sb[t][:, cols],
                    in_=y_bank[(t, s)][:],
                    func=ACT.Square,
                    bias=negc[t][:],
                    accum_out=sqs[t][:, s : s + 1],
                )

        def upper_means():
            nc.scalar.copy(out=acc_sb[:], in_=acc[:, 0:256])
            bank = ps_y.tile([P, 512], F32, name="mean_bank", tag="y")
            for t in range(2):
                nc.tensor.matmul(
                    out=bank[:, t : t + 1], lhsT=acc_sb[:, P * t : P * t + P], rhs=minus_nth[:], start=True, stop=True
                )
            y_bank["mean"] = bank

        def upper_means_out():
            bank = y_bank["mean"]
            for t in range(2):
                nc.scalar.activation(out=dsq[t][:], in_=bank[:, t : t + 1], func=ACT.Square, bias=posc[t][:])
            for t in range(2):
                nc.scalar.activation(out=ngm[t][:], in_=bank[:, t : t + 1], func=ACT.Identity, scale=gb[:, t : t + 1])

        def relu_bank(t, s):
            nc.scalar.activation(
                out=y_sb[t][:, 512 * s : 512 * s + 512],
                in_=y_bank[(t, s)][:],
                func=ACT.Relu,
                scale=scl[t][:],
                bias=bia[t][:],
            )

        def relu_last(h):
            lo = 1536 + 256 * h
            nc.scalar.activation(
                out=y_sb[2][:, lo : lo + 256],
                in_=y_bank[("last", h)][:, 0:256],
                func=ACT.Relu,
                scale=scl[2][:],
                bias=bia[2][:],
            )

        def take_out(a, s):
            cols = slice(512 * s, 512 * s + 512)
            for t in o_tiles(a):
                nc.scalar.activation(
                    out=y_sb[t][:, cols], in_=y_bank[(t, s)][:], func=ACT.Identity, accum_out=sums[t][:, s : s + 1]
                )
            if s == 0:
                for t in o_tiles(a):
                    nc.scalar.activation(out=negc[t][:], in_=sums[t][:, 0:1], func=ACT.Identity, scale=-1.0 / 512.0)
            for t in o_tiles(a):
                nc.scalar.activation(
                    out=o_sb[t][:, cols],
                    in_=y_bank[(t, s)][:],
                    func=ACT.Square,
                    bias=negc[t][:],
                    accum_out=sqs[t][:, s : s + 1],
                )

        def lower_part_stats():
            nc.scalar.activation(
                out=junk_a[2][:, 0:3], in_=sums[2][:, 0:3], func=ACT.Identity, scale=1.0 / 1536.0, accum_out=stats2[:, 1:2]
            )
            nc.scalar.activation(
                out=junk_b[2][:, 0:3], in_=sqs[2][:, 0:3], func=ACT.Identity, accum_out=msq[2][:]
            )
            nc.scalar.activation(out=dsq[2][:], in_=stats2[:, 1:2], func=ACT.Square, bias=negc[2][:])
            nc.scalar.activation(
                out=stats2[:, 2:3], in_=dsq[2][:], func=ACT.Identity, scale=-1536.0, bias=msq[2][:]
            )

        def lower_stats():
            for h in range(2):
                nc.vector.bn_stats(out=stats2[:, 3 + 6 * h : 9 + 6 * h], in_=y_bank[("last", h)][:, 0:256])
            average(1, 384, 256)
            store(1, 384, 256)
            nc.vector.bn_aggr(out=mv2[:], in_=stats2[:])
            nc.scalar.activation(out=rstd[2][:], in_=mv2[:, 1:2], func=ACT.Abs_reciprocal_sqrt, bias=eps1[:])
            nc.scalar.activation(out=ngm[2][:], in_=mv2[:, 0:1], func=ACT.Identity, scale=ngam[:])
            nc.scalar.activation(out=scl[2][:], in_=gb[:, 2:3], func=ACT.Identity, scale=rstd[2][:])
            nc.scalar.activation(out=bia[2][:], in_=ngm[2][:], func=ACT.Identity, scale=rstd[2][:], bias=gb[:, 5:6])

        def statistics(tiles):
            for t in tiles:
                nc.scalar.activation(
                    out=junk_b[t][:],
                    in_=sqs[t][:],
                    func=ACT.Identity,
                    scale=1.0 / NPIX,
                    bias=eps4[:],
                    accum_out=msq[t][:],
                )
            for t in tiles:
                nc.scalar.activation(
                    out=rstd[t][:], in_=dsq[t][:], func=ACT.Abs_reciprocal_sqrt, scale=-1.0, bias=msq[t][:]
                )
            for t in tiles:
                nc.scalar.activation(out=scl[t][:], in_=gb[:, t : t + 1], func=ACT.Identity, scale=rstd[t][:])
            for t in tiles:
                nc.scalar.activation(
                    out=bia[t][:], in_=ngm[t][:], func=ACT.Identity, scale=rstd[t][:], bias=gb[:, 3 + t : 4 + t]
                )

        def relu(t, lo, n):
            nc.scalar.activation(
                out=y_sb[t][:, lo : lo + n], in_=y_sb[t][:, lo : lo + n], func=ACT.Relu, scale=scl[t][:], bias=bia[t][:]
            )

        def average(t, lo, n):
            b, w0 = divmod(lo, 1024)
            nc.vector.scalar_tensor_tensor(
                out=o_sb[t][:, lo : lo + n],
                in0=pn[t][:, b, w0 : w0 + n],
                scalar=0.5,
                in1=y_sb[t][:, lo : lo + n],
                op0=ALU.mult,
                op1=ALU.add,
            )

        def pe_average(t, lo, n):
            b, w0 = divmod(lo, 1024)
            bank = ps_att.tile([P, 512], F32, name="add_bank", tag="att")
            nc.tensor.matmul(out=bank[:, 0:n], lhsT=half_i[:], rhs=pn[t][:, b, w0 : w0 + n], start=True, stop=False)
            nc.tensor.matmul(out=bank[:, 0:n], lhsT=ident_f[:], rhs=y_sb[t][:, lo : lo + n], start=False, stop=True)
            y_bank[("add", t, lo)] = bank

        def pe_average_out(t, lo, n):
            nc.scalar.copy(out=o_sb[t][:, lo : lo + n], in_=y_bank[("add", t, lo)][:, 0:n])

        def store(t, lo, n):
            b, w0 = divmod(lo, 1024)
            for jj in range(2):
                nc.sync.dma_start(
                    out=out[1 + 2 * t + jj, b].rearrange("c h w -> c (h w)")[:, w0 : w0 + n],
                    in_=o_sb[t][jj:P:2, lo : lo + n],
                )

        def node0_sum(h):
            bank = ps_y.tile([P, 512], F32, name="o0_bank", tag="y")
            nc.tensor.matmul(out=bank[:], lhsT=half_i[:], rhs=h0[:, 512 * h : 512 * h + 512], start=True, stop=False)
            nc.tensor.matmul(out=bank[:], lhsT=half_i[:], rhs=p0[:, 512 * h : 512 * h + 512], start=False, stop=True)
            y_bank[("o0", h)] = bank

        def node0_out(h):
            nc.scalar.copy(out=o0[:, 512 * h : 512 * h + 512], in_=y_bank[("o0", h)][:])

        acc = ps_acc.tile([P, 512], F32, name="acc")
        att_bank[(0, 0)], att_bank[(1, 0)] = first_banks
        gpsimd_share(0, 416, 96)
        for i in range(1, 8):
            gpsimd_share(i, 0, G_SHARE[i])
        regroup_runs(nc.scalar.copy, 1, G_SHARE[1], 512 - G_SHARE[1])
        nc.scalar.copy(out=att_p[:], in_=att_t[:, 0:P])
        for i in range(2, 4):
            regroup_runs(nc.scalar.copy, i, G_SHARE[i], 512 - G_SHARE[i])
        spread_att(0, 1)
        for c in range(2):
            regroup_runs(nc.vector.tensor_copy, 0, 128 * c, 128)
        for c in range(2):
            multiply(0, 0, 128 * c, 128)
        multiply(0, 0, 256, 256)
        multiply(1, 0)
        multiply(0, 1)
        for t in range(3):
            w_transpose(t)
        for t in range(3):
            w_copy(t)
        gains()
        spread_att(0, 2)
        multiply(1, 1)
        quantise(0)
        regroup_runs(nc.scalar.copy, 4, G_SHARE[4], 512 - G_SHARE[4])
        regroup_runs(nc.scalar.copy, 5, G_SHARE[5], 512 - G_SHARE[5])
        spread_att(0, 3)
        multiply(2, 0)
        w_quantise(0, 512)
        convolve(0, 0)
        quantise(1)
        multiply(2, 1)
        regroup_runs(nc.scalar.copy, 6, G_SHARE[6], 512 - G_SHARE[6])
        upper_squares(0)
        regroup_runs(nc.scalar.copy, 7, G_SHARE[7], 512 - G_SHARE[7])
        spread_att(1, 1)
        multiply(3, 0)
        quantise(2)
        multiply(3, 1)
        w_quantise(512, 256)
        convolve(0, 1)
        upper_squares(1)
        convolve(1, 0)
        take_out(1, 0)
        spread_att(1, 2)
        multiply(4, 0)
        quantise(3)
        multiply(4, 1)
        convolve(0, 2)
        upper_squares(2)
        node0_sum(0)
        node0_sum(1)
        node0_out(0)
        node0_out(1)
        nc.sync.dma_start(out=out[0].rearrange("b c h w -> (b c) (h w)"), in_=o0[:])
        spread_att(1, 3)
        multiply(5, 0)
        quantise(4)
        multiply(5, 1)
        convolve(0, 3)
        upper_means()
        upper_squares(3)
        upper_means_out()
        statistics((0, 1))
        convolve_tile(0, 0, 0)
        convolve_tile(0, 0, 1)
        relu_bank(0, 0)
        relu_bank(0, 1)
        convolve_tile(0, 0, 2)
        convolve_tile(0, 0, 3)
        multiply(6, 0)
        quantise(5)
        multiply(6, 1)
        convolve(1, 1)
        relu_bank(0, 2)
        relu_bank(0, 3)
        take_out(1, 1)
        convolve_tile(1, 0, 0)
        convolve_tile(1, 0, 1)
        multiply(7, 0)
        quantise(6)
        multiply(7, 1)
        relu_bank(1, 0)
        relu_bank(1, 1)
        convolve(1, 2)
        convolve_tile(1, 0, 2)
        convolve_tile(1, 0, 3)
        take_out(1, 2)
        pe_average(0, 1664, 384)
        lower_part_stats()
        relu_bank(1, 2)
        pe_average_out(0, 1664, 384)
        relu_bank(1, 3)
        average(0, 0, 1024)
        store(0, 0, 1024)
        average(0, 1024, 640)
        store(0, 1024, 640)
        quantise(7)
        convolve_last()
        average(1, 0, 384)
        store(1, 0, 384)
        store(0, 1664, 384)
        lower_stats()
        average(1, 640, 384)
        store(1, 640, 384)
        average(1, 1024, 512)
        store(1, 1024, 512)
        average(1, 1536, 512)
        store(1, 1536, 512)
        for c in range(3):
            relu(2, 512 * c, 512)
        for h in range(2):
            relu_last(h)
        for lo, n in ((0, 512), (512, 512), (1024, 512), (1536, 256), (1792, 256)):
            average(2, lo, n)
            store(2, lo, n)
